import numpy as np
import ml_dtypes


def mxq(x, axis, fmt="e4m3"):
    dtype, down = {"e4m3": (ml_dtypes.float8_e4m3fn, 7), "e5m2": (ml_dtypes.float8_e5m2, 14)}[fmt]
    v = np.moveaxis(np.asarray(x, np.float32).astype(ml_dtypes.bfloat16).astype(np.float64), axis, -1)
    blocks = v.reshape(v.shape[:-1] + (-1, 32))
    amax = np.abs(blocks).max(-1, keepdims=True)
    byte = np.maximum(np.where(amax > 0, np.frexp(amax)[1] - 1 + 127, 0) - down, 1)
    scale = np.exp2(byte - 127.0)
    codes = (blocks / scale).astype(np.float32).astype(dtype).astype(np.float64)
    return np.moveaxis((codes * scale).reshape(v.shape), -1, axis)


WIDE = False


def mx_kscale(k):
    if not WIDE:
        return np.ones(k)
    levels = np.array([10, -10, 5, -5, 0])
    a = np.random.permutation(np.resize(levels, k // 512 * 4)).reshape(k // 512, 4)
    idx = np.arange(k)
    return np.exp2(a[idx // 512, idx % 128 // 32])


BF16 = ml_dtypes.bfloat16


def bf(x):
    return np.asarray(x, np.float32).astype(BF16)


def f64(x):
    return np.asarray(x).astype(np.float64)


B, P, K, D, L, C0, C1, C2, C3 = 8192, 64, 128, 512, 4, 256, 512, 1024, 512
C = C3
F = 2 * C
EPS = 1e-5


def layernorm(x, g, b):
    m = x.mean(axis=-1, keepdims=True)
    v = x.var(axis=-1, keepdims=True)
    return (x - m) / np.sqrt(v + EPS) * g + b


def l2norm(x):
    n = np.sqrt((x * x).sum(axis=-1, keepdims=True))
    return x / np.maximum(n, 1e-12)


def setup_inputs():
    s = mx_kscale(F)
    return {"pooled": bf(0.5 + 2.0 * np.random.standard_normal((B, C))),
            "proto": bf(np.random.standard_normal((1, C)) + np.random.standard_normal((P, C))),
            "ln_g": bf((1.0 + 0.1 * np.random.standard_normal(F)) * s),
            "ln_b": bf(0.1 * np.random.standard_normal(F) * s),
            "W": bf(np.random.standard_normal((F, D)) / np.sqrt(F) / s[:, None]),
            "b": bf(0.1 * np.random.standard_normal(D))}


def reference(pooled, proto, ln_g, ln_b, W, b):
    pl = f64(pooled)
    proto_ctx = np.broadcast_to(f64(proto).mean(axis=0, keepdims=True), pl.shape)
    fused = np.concatenate([pl, proto_ctx], axis=1)
    z = layernorm(fused, f64(ln_g), f64(ln_b))
    h = np.maximum((mxq(z, 1, "e4m3") @ mxq(f64(W), 0, "e4m3")) + f64(b), 0.0)
    return l2norm(h)

@@ -1,0 +1,289 @@
+from contextlib import ExitStack
+
+import concourse.mybir as mybir
+from concourse.masks import make_identity
+
+F32 = mybir.dt.float32
+BF16 = mybir.dt.bfloat16
+U32 = mybir.dt.uint32
+U8 = mybir.dt.uint8
+FP8X4 = mybir.dt.float8_e4m3fn_x4
+ALU = mybir.AluOpType
+ACT = mybir.ActivationFunctionType
+
+P = 128
+PACK = 4
+K_PASS = P * PACK
+
+ROWS = 8192
+CHANNELS = 512
+FEATURES = 2 * CHANNELS
+D_OUT = 512
+PROTOS = 64
+PASSES = FEATURES // K_PASS
+BLOCKS = FEATURES // P
+TILES = 4
+GROUP_ROWS = TILES * P
+GROUPS = ROWS // GROUP_ROWS
+STATS = 6
+LN_EPS = 1e-5
+NORM_FLOOR = 1e-12
+FIRST_STAGE_LEAD = 4
+LAST_STAGE_LAG = 4
+
+FLOPS = 2 * ROWS * FEATURES * D_OUT
+
+
+def side_by_side(nc, grouped, planes):
+    nc.vector.tensor_copy(
+        out=grouped.rearrange("p (c i) t -> p c t i", i=4),
+        in_=planes.rearrange("p t (c i) -> p c t i", i=4),
+    )
+
+
+def tile_textguidedcamfusion_pa_t_kernel(tc, pooled, proto, ln_g, ln_b, W, b, out):
+    nc = tc.nc
+    with ExitStack() as stack:
+        const = stack.enter_context(tc.tile_pool(name="const", bufs=1))
+        x_pool = stack.enter_context(tc.tile_pool(name="x", bufs=5))
+        small = stack.enter_context(tc.tile_pool(name="small", bufs=4))
+        u_pool = stack.enter_context(tc.tile_pool(name="u", bufs=3))
+        z_pool = stack.enter_context(tc.tile_pool(name="z", bufs=2))
+        q_pool = stack.enter_context(tc.tile_pool(name="q", bufs=3))
+        h_pool = stack.enter_context(tc.tile_pool(name="h", bufs=2))
+        junk_pool = stack.enter_context(tc.tile_pool(name="junk", bufs=1))
+        o_pool = stack.enter_context(tc.tile_pool(name="o", bufs=2))
+        psum_t = stack.enter_context(tc.psum_pool(name="psum_t", bufs=4))
+        psum_acc = stack.enter_context(tc.psum_pool(name="psum_acc", bufs=4))
+
+        identity = const.tile([P, P], F32)
+        make_identity(nc, identity[:])
+        ones = const.tile([P, P], BF16)
+        nc.vector.memset(ones[:], 1.0)
+        eps = const.tile([P, 1], F32)
+        nc.vector.memset(eps[:], LN_EPS)
+
+        proto_rows = const.tile([P, CHANNELS], BF16)
+        nc.vector.memset(proto_rows[:], 0.0)
+        nc.sync.dma_start(out=proto_rows[0:PROTOS, :], in_=proto)
+        proto_sum = psum_acc.tile([P, CHANNELS], F32, tag="acc")
+        nc.tensor.matmul(proto_sum[:], lhsT=ones[:], rhs=proto_rows[:], start=True, stop=True)
+        context = const.tile([P, CHANNELS], F32)
+        nc.vector.tensor_scalar_mul(out=context[:], in0=proto_sum[:], scalar1=1.0 / PROTOS)
+
+        context_stats = const.tile([P, STATS], F32)
+        nc.vector.bn_stats(out=context_stats[:], in_=context[:])
+        stats = const.tile([P, GROUPS * TILES, 2, STATS], F32)
+        nc.vector.tensor_copy(
+            out=stats[:, :, 1, :],
+            in_=context_stats[:].unsqueeze(1).to_broadcast([P, GROUPS * TILES, STATS]),
+        )
+
+        affine_rows = const.tile([P, P], BF16)
+        nc.vector.memset(affine_rows[:], 0.0)
+        nc.sync.dma_start(out=affine_rows[0:BLOCKS, :], in_=ln_g.rearrange("(q p) -> q p", p=P))
+        nc.sync.dma_start(
+            out=affine_rows[BLOCKS : 2 * BLOCKS, :], in_=ln_b.rearrange("(q p) -> q p", p=P)
+        )
+        affine_rows_f32 = const.tile([P, P], F32)
+        nc.vector.tensor_copy(out=affine_rows_f32[:], in_=affine_rows[:])
+        affine_cols = psum_t.tile([P, P], F32, tag="ut")
+        nc.tensor.transpose(affine_cols[:], affine_rows_f32[:], identity[:])
+        gain_shift = const.tile([P, 2 * BLOCKS], F32)
+        nc.vector.tensor_copy(out=gain_shift[:], in_=affine_cols[:, 0 : 2 * BLOCKS])
+
+        bias_rows = const.tile([P, D_OUT], BF16)
+        nc.vector.memset(bias_rows[:], 0.0)
+        nc.sync.dma_start(out=bias_rows[0:1, :], in_=b.rearrange("(o d) -> o d", o=1))
+        bias_sum = psum_acc.tile([P, D_OUT], F32, tag="acc")
+        nc.tensor.matmul(bias_sum[:], lhsT=ones[:], rhs=bias_rows[:], start=True, stop=True)
+        bias = const.tile([P, D_OUT], F32)
+        nc.vector.tensor_copy(out=bias[:], in_=bias_sum[:])
+
+        w_planes = const.tile([P, PASSES, PACK, D_OUT], BF16)
+        nc.sync.dma_start(
+            out=w_planes[:], in_=W.rearrange("(g t p) d -> p g t d", t=PACK, p=P)
+        )
+        w_grouped = const.tile([P, PASSES, D_OUT, PACK], BF16, align_bytes=64)
+        w_codes = const.tile([P, PASSES, D_OUT], U32, align_bytes=64)
+        w_scales = const.tile([P, PASSES, D_OUT], U8, align_bytes=64)
+        for g in range(PASSES):
+            side_by_side(nc, w_grouped[:, g], w_planes[:, g])
+        for g in range(PASSES):
+            nc.vector.quantize_mx(
+                out=w_codes[:, g, :].bitcast(FP8X4),
+                scales=w_scales[:, g, :],
+                in_=w_grouped[:, g].rearrange("p d t -> p (d t)"),
+            )
+
+        x_of, mean_var_of, std_of, rstd_of, neg_mean_of, u_of = {}, {}, {}, {}, {}, {}
+        planes_of, codes_of, scales_of, acc_of, h_of, relu_of = {}, {}, {}, {}, {}, {}
+        sum_squares_of, floored_of, norm_of = {}, {}, {}
+
+        def rows_of(group):
+            return slice(group * GROUP_ROWS, (group + 1) * GROUP_ROWS)
+
+        def load_rows(group):
+            x = x_pool.tile([P, TILES, CHANNELS], BF16)
+            nc.sync.dma_start(
+                out=x[:], in_=pooled[rows_of(group), :].rearrange("(p r) k -> p r k", r=TILES)
+            )
+            x_of[group] = x
+
+        def row_statistics(group):
+            mean_var = small.tile([P, TILES, 2], F32)
+            for r in range(TILES):
+                nc.vector.bn_stats(out=stats[:, group * TILES + r, 0, :], in_=x_of[group][:, r, :])
+            for r in range(TILES):
+                nc.vector.bn_aggr(
+                    out=mean_var[:, r, :],
+                    in_=stats[:, group * TILES + r, :, :].rearrange("p a s -> p (a s)"),
+                )
+            mean_var_of[group] = mean_var
+
+        def root_of_variance(group):
+            std = small.tile([P, TILES], F32)
+            nc.scalar.activation(
+                out=std[:], in_=mean_var_of[group][:, :, 1], func=ACT.Sqrt, bias=eps[:]
+            )
+            std_of[group] = std
+
+        def invert_std(group):
+            rstd = small.tile([P, TILES], F32)
+            nc.vector.reciprocal(out=rstd[:], in_=std_of[group][:])
+            neg_mean = small.tile([P, TILES], F32)
+            nc.vector.tensor_scalar_mul(
+                out=neg_mean[:], in0=mean_var_of[group][:, :, 0], scalar1=-1.0
+            )
+            rstd_of[group] = rstd
+            neg_mean_of[group] = neg_mean
+
+        def normalise(group):
+            u = u_pool.tile([P, TILES, FEATURES], F32)
+            for r in range(TILES):
+                for half, source in ((0, x_of[group][:, r, :]), (1, context[:])):
+                    nc.gpsimd.tensor_scalar(
+                        out=u[:, r, half * CHANNELS : (half + 1) * CHANNELS],
+                        in0=source,
+                        scalar1=neg_mean_of[group][:, r : r + 1],
+                        scalar2=rstd_of[group][:, r : r + 1],
+                        op0=ALU.add,
+                        op1=ALU.mult,
+                    )
+            u_of[group] = u
+
+        def transpose_and_scale(group):
+            z_planes = z_pool.tile([P, PASSES, PACK, GROUP_ROWS], BF16)
+            for block in range(BLOCKS):
+                ut = psum_t.tile([P, TILES, P], F32, tag="ut")
+                for r in range(TILES):
+                    nc.tensor.transpose(
+                        ut[:, r, :], u_of[group][:, r, block * P : (block + 1) * P], identity[:]
+                    )
+                nc.scalar.activation(
+                    out=z_planes[:, block // PACK, block % PACK, :],
+                    in_=ut[:].rearrange("p r i -> p (r i)"),
+                    func=ACT.Identity,
+                    scale=gain_shift[:, block : block + 1],
+                    bias=gain_shift[:, BLOCKS + block : BLOCKS + block + 1],
+                )
+            planes_of[group] = z_planes
+
+        def quantise(group):
+            z_grouped = z_pool.tile([P, PASSES, GROUP_ROWS, PACK], BF16, align_bytes=64)
+            z_codes = q_pool.tile([P, PASSES, GROUP_ROWS], U32, align_bytes=64)
+            z_scales = q_pool.tile([P, PASSES, GROUP_ROWS], U8, align_bytes=64)
+            for g in range(PASSES):
+                side_by_side(nc, z_grouped[:, g], planes_of[group][:, g])
+            for g in range(PASSES):
+                nc.vector.quantize_mx(
+                    out=z_codes[:, g, :].bitcast(FP8X4),
+                    scales=z_scales[:, g, :],
+                    in_=z_grouped[:, g].rearrange("p c t -> p (c t)"),
+                )
+            codes_of[group] = z_codes
+            scales_of[group] = z_scales
+
+        def multiply(group):
+            for r in range(TILES):
+                tile_cols = slice(r * P, (r + 1) * P)
+                acc = psum_acc.tile([P, D_OUT], F32, tag="acc")
+                for g in range(PASSES):
+                    nc.tensor.matmul_mx(
+                        out=acc[:],
+                        lhsT=codes_of[group][:, g, tile_cols].bitcast(FP8X4),
+                        lhsT_scale=scales_of[group][:, g, tile_cols],
+                        rhs=w_codes[:, g, :].bitcast(FP8X4),
+                        rhs_scale=w_scales[:, g, :],
+                        start=(g == 0),
+                        stop=(g == PASSES - 1),
+                    )
+                acc_of[group, r] = acc
+
+        def add_bias(group):
+            h = h_pool.tile([P, TILES, D_OUT], F32)
+            for r in range(TILES):
+                nc.vector.tensor_tensor(
+                    out=h[:, r, :], in0=acc_of[group, r][:], in1=bias[:], op=ALU.add
+                )
+            h_of[group] = h
+
+        def relu_and_squares(group):
+            relu = h_pool.tile([P, TILES, D_OUT], F32)
+            squares = junk_pool.tile([P, TILES, D_OUT], F32)
+            sum_squares = small.tile([P, TILES], F32)
+            for r in range(TILES):
+                nc.scalar.activation(out=relu[:, r, :], in_=h_of[group][:, r, :], func=ACT.Relu)
+            for r in range(TILES):
+                nc.scalar.activation(
+                    out=squares[:, r, :],
+                    in_=relu[:, r, :],
+                    func=ACT.Square,
+                    accum_out=sum_squares[:, r : r + 1],
+                )
+            relu_of[group] = relu
+            sum_squares_of[group] = sum_squares
+
+        def floor_squares(group):
+            floored = small.tile([P, TILES], F32)
+            nc.vector.tensor_scalar_max(
+                out=floored[:], in0=sum_squares_of[group][:], scalar1=NORM_FLOOR * NORM_FLOOR
+            )
+            floored_of[group] = floored
+
+        def root_of_squares(group):
+            norm = small.tile([P, TILES], F32)
+            nc.scalar.activation(out=norm[:], in_=floored_of[group][:], func=ACT.Sqrt)
+            norm_of[group] = norm
+
+        def store_unit_rows(group):
+            inv_norm = small.tile([P, TILES], F32)
+            nc.vector.reciprocal(out=inv_norm[:], in_=norm_of[group][:])
+            unit = o_pool.tile([P, TILES, D_OUT], F32)
+            for r in range(TILES):
+                nc.vector.tensor_scalar_mul(
+                    out=unit[:, r, :], in0=relu_of[group][:, r, :], scalar1=inv_norm[:, r : r + 1]
+                )
+            nc.sync.dma_start(
+                out=out[rows_of(group), :].rearrange("(p r) d -> p r d", r=TILES), in_=unit[:]
+            )
+
+        def run(stage, group):
+            if 0 <= group < GROUPS:
+                stage(group)
+
+        with tc.manual_schedule():
+            for step in range(-FIRST_STAGE_LEAD, GROUPS + LAST_STAGE_LAG):
+                run(load_rows, step + FIRST_STAGE_LEAD)
+                run(root_of_variance, step + 2)
+                run(root_of_squares, step - LAST_STAGE_LAG)
+                run(multiply, step - 2)
+                run(relu_and_squares, step - 3)
+                run(transpose_and_scale, step)
+                run(normalise, step + 1)
+                run(quantise, step - 1)
+                run(add_bias, step - 2)
+                run(invert_std, step + 2)
+                run(floor_squares, step - 3)
+                run(store_unit_rows, step - LAST_STAGE_LAG)
+                run(row_statistics, step + 3)

@@ -261,8 +261,13 @@ def tile_textguidedcamfusion_pa_t_kernel(tc, pooled, proto, ln_g, ln_b, W, b, ou
             nc.vector.reciprocal(out=inv_norm[:], in_=norm_of[group][:])
             unit = o_pool.tile([P, TILES, D_OUT], F32)
             for r in range(TILES):
-                nc.vector.tensor_scalar_mul(
-                    out=unit[:, r, :], in0=relu_of[group][:, r, :], scalar1=inv_norm[:, r : r + 1]
+                nc.gpsimd.tensor_scalar(
+                    out=unit[:, r, :],
+                    in0=relu_of[group][:, r, :],
+                    scalar1=inv_norm[:, r : r + 1],
+                    scalar2=0.0,
+                    op0=ALU.mult,
+                    op1=ALU.add,
                 )
             nc.sync.dma_start(
                 out=out[rows_of(group), :].rearrange("(p r) d -> p r d", r=TILES), in_=unit[:]

@@ -30,6 +30,8 @@ LN_EPS = 1e-5
 NORM_FLOOR = 1e-12
 FIRST_STAGE_LEAD = 4
 LAST_STAGE_LAG = 4
+WEIGHTS_LOAD_STEP = -3
+WEIGHTS_QUANTISE_STEP = 0
 
 FLOPS = 2 * ROWS * FEATURES * D_OUT
 
@@ -101,20 +103,24 @@ def tile_textguidedcamfusion_pa_t_kernel(tc, pooled, proto, ln_g, ln_b, W, b, ou
         nc.vector.tensor_copy(out=bias[:], in_=bias_sum[:])
 
         w_planes = const.tile([P, PASSES, PACK, D_OUT], BF16)
-        nc.sync.dma_start(
-            out=w_planes[:], in_=W.rearrange("(g t p) d -> p g t d", t=PACK, p=P)
-        )
         w_grouped = const.tile([P, PASSES, D_OUT, PACK], BF16, align_bytes=64)
         w_codes = const.tile([P, PASSES, D_OUT], U32, align_bytes=64)
         w_scales = const.tile([P, PASSES, D_OUT], U8, align_bytes=64)
-        for g in range(PASSES):
-            side_by_side(nc, w_grouped[:, g], w_planes[:, g])
-        for g in range(PASSES):
-            nc.vector.quantize_mx(
-                out=w_codes[:, g, :].bitcast(FP8X4),
-                scales=w_scales[:, g, :],
-                in_=w_grouped[:, g].rearrange("p d t -> p (d t)"),
+
+        def load_weights():
+            nc.sync.dma_start(
+                out=w_planes[:], in_=W.rearrange("(g t p) d -> p g t d", t=PACK, p=P)
             )
+
+        def quantise_weights():
+            for g in range(PASSES):
+                side_by_side(nc, w_grouped[:, g], w_planes[:, g])
+            for g in range(PASSES):
+                nc.vector.quantize_mx(
+                    out=w_codes[:, g, :].bitcast(FP8X4),
+                    scales=w_scales[:, g, :],
+                    in_=w_grouped[:, g].rearrange("p d t -> p (d t)"),
+                )
 
         x_of, mean_var_of, std_of, rstd_of, neg_mean_of, u_of = {}, {}, {}, {}, {}, {}
         planes_of, codes_of, scales_of, acc_of, h_of, relu_of = {}, {}, {}, {}, {}, {}
@@ -146,17 +152,15 @@ def tile_textguidedcamfusion_pa_t_kernel(tc, pooled, proto, ln_g, ln_b, W, b, ou
             nc.scalar.activation(
                 out=std[:], in_=mean_var_of[group][:, :, 1], func=ACT.Sqrt, bias=eps[:]
             )
+            neg_mean = small.tile([P, TILES], F32)
+            nc.scalar.mul(out=neg_mean[:], in_=mean_var_of[group][:, :, 0], mul=-1.0)
             std_of[group] = std
+            neg_mean_of[group] = neg_mean
 
         def invert_std(group):
             rstd = small.tile([P, TILES], F32)
             nc.vector.reciprocal(out=rstd[:], in_=std_of[group][:])
-            neg_mean = small.tile([P, TILES], F32)
-            nc.vector.tensor_scalar_mul(
-                out=neg_mean[:], in0=mean_var_of[group][:, :, 0], scalar1=-1.0
-            )
             rstd_of[group] = rstd
-            neg_mean_of[group] = neg_mean
 
         def normalise(group):
             u = u_pool.tile([P, TILES, FEATURES], F32)
@@ -260,18 +264,12 @@ def tile_textguidedcamfusion_pa_t_kernel(tc, pooled, proto, ln_g, ln_b, W, b, ou
             inv_norm = small.tile([P, TILES], F32)
             nc.vector.reciprocal(out=inv_norm[:], in_=norm_of[group][:])
             unit = o_pool.tile([P, TILES, D_OUT], F32)
+            out_rows = out[rows_of(group), :].rearrange("(p r) d -> p r d", r=TILES)
             for r in range(TILES):
-                nc.gpsimd.tensor_scalar(
-                    out=unit[:, r, :],
-                    in0=relu_of[group][:, r, :],
-                    scalar1=inv_norm[:, r : r + 1],
-                    scalar2=0.0,
-                    op0=ALU.mult,
-                    op1=ALU.add,
+                nc.vector.tensor_scalar_mul(
+                    out=unit[:, r, :], in0=relu_of[group][:, r, :], scalar1=inv_norm[:, r : r + 1]
                 )
-            nc.sync.dma_start(
-                out=out[rows_of(group), :].rearrange("(p r) d -> p r d", r=TILES), in_=unit[:]
-            )
+                nc.sync.dma_start(out=out_rows[:, r, :], in_=unit[:, r, :])
 
         def run(stage, group):
             if 0 <= group < GROUPS:
@@ -280,15 +278,19 @@ def tile_textguidedcamfusion_pa_t_kernel(tc, pooled, proto, ln_g, ln_b, W, b, ou
         with tc.manual_schedule():
             for step in range(-FIRST_STAGE_LEAD, GROUPS + LAST_STAGE_LAG):
                 run(load_rows, step + FIRST_STAGE_LEAD)
-                run(root_of_variance, step + 2)
-                run(root_of_squares, step - LAST_STAGE_LAG)
+                if step == WEIGHTS_LOAD_STEP:
+                    load_weights()
                 run(multiply, step - 2)
                 run(relu_and_squares, step - 3)
+                run(root_of_variance, step + 2)
+                run(root_of_squares, step - LAST_STAGE_LAG)
                 run(transpose_and_scale, step)
                 run(normalise, step + 1)
-                run(quantise, step - 1)
+                run(row_statistics, step + 3)
+                if step == WEIGHTS_QUANTISE_STEP:
+                    quantise_weights()
                 run(add_bias, step - 2)
+                run(quantise, step - 1)
                 run(invert_std, step + 2)
                 run(floor_squares, step - 3)
                 run(store_unit_rows, step - LAST_STAGE_LAG)
-                run(row_statistics, step + 3)

@@ -26,12 +26,11 @@ TILES = 4
 GROUP_ROWS = TILES * P
 GROUPS = ROWS // GROUP_ROWS
 STATS = 6
+SCALAR_TILES = 1
 LN_EPS = 1e-5
 NORM_FLOOR = 1e-12
 FIRST_STAGE_LEAD = 4
 LAST_STAGE_LAG = 4
-WEIGHTS_LOAD_STEP = -3
-WEIGHTS_QUANTISE_STEP = 0
 
 FLOPS = 2 * ROWS * FEATURES * D_OUT
 
@@ -103,28 +102,24 @@ def tile_textguidedcamfusion_pa_t_kernel(tc, pooled, proto, ln_g, ln_b, W, b, ou
         nc.vector.tensor_copy(out=bias[:], in_=bias_sum[:])
 
         w_planes = const.tile([P, PASSES, PACK, D_OUT], BF16)
+        nc.sync.dma_start(
+            out=w_planes[:], in_=W.rearrange("(g t p) d -> p g t d", t=PACK, p=P)
+        )
         w_grouped = const.tile([P, PASSES, D_OUT, PACK], BF16, align_bytes=64)
         w_codes = const.tile([P, PASSES, D_OUT], U32, align_bytes=64)
         w_scales = const.tile([P, PASSES, D_OUT], U8, align_bytes=64)
-
-        def load_weights():
-            nc.sync.dma_start(
-                out=w_planes[:], in_=W.rearrange("(g t p) d -> p g t d", t=PACK, p=P)
+        for g in range(PASSES):
+            side_by_side(nc, w_grouped[:, g], w_planes[:, g])
+        for g in range(PASSES):
+            nc.vector.quantize_mx(
+                out=w_codes[:, g, :].bitcast(FP8X4),
+                scales=w_scales[:, g, :],
+                in_=w_grouped[:, g].rearrange("p d t -> p (d t)"),
             )
-
-        def quantise_weights():
-            for g in range(PASSES):
-                side_by_side(nc, w_grouped[:, g], w_planes[:, g])
-            for g in range(PASSES):
-                nc.vector.quantize_mx(
-                    out=w_codes[:, g, :].bitcast(FP8X4),
-                    scales=w_scales[:, g, :],
-                    in_=w_grouped[:, g].rearrange("p d t -> p (d t)"),
-                )
 
         x_of, mean_var_of, std_of, rstd_of, neg_mean_of, u_of = {}, {}, {}, {}, {}, {}
         planes_of, codes_of, scales_of, acc_of, h_of, relu_of = {}, {}, {}, {}, {}, {}
-        sum_squares_of, floored_of, norm_of = {}, {}, {}
+        sum_squares_of, floored_of, norm_of, shift_of = {}, {}, {}, {}
 
         def rows_of(group):
             return slice(group * GROUP_ROWS, (group + 1) * GROUP_ROWS)
@@ -152,28 +147,45 @@ def tile_textguidedcamfusion_pa_t_kernel(tc, pooled, proto, ln_g, ln_b, W, b, ou
             nc.scalar.activation(
                 out=std[:], in_=mean_var_of[group][:, :, 1], func=ACT.Sqrt, bias=eps[:]
             )
-            neg_mean = small.tile([P, TILES], F32)
-            nc.scalar.mul(out=neg_mean[:], in_=mean_var_of[group][:, :, 0], mul=-1.0)
             std_of[group] = std
-            neg_mean_of[group] = neg_mean
 
         def invert_std(group):
             rstd = small.tile([P, TILES], F32)
             nc.vector.reciprocal(out=rstd[:], in_=std_of[group][:])
+            neg_mean = small.tile([P, TILES], F32)
+            nc.vector.tensor_scalar_mul(
+                out=neg_mean[:], in0=mean_var_of[group][:, :, 0], scalar1=-1.0
+            )
+            shift = small.tile([P, SCALAR_TILES], F32)
+            nc.vector.tensor_mul(
+                out=shift[:], in0=neg_mean[:, 0:SCALAR_TILES], in1=rstd[:, 0:SCALAR_TILES]
+            )
             rstd_of[group] = rstd
+            neg_mean_of[group] = neg_mean
+            shift_of[group] = shift
 
         def normalise(group):
             u = u_pool.tile([P, TILES, FEATURES], F32)
             for r in range(TILES):
                 for half, source in ((0, x_of[group][:, r, :]), (1, context[:])):
-                    nc.gpsimd.tensor_scalar(
-                        out=u[:, r, half * CHANNELS : (half + 1) * CHANNELS],
-                        in0=source,
-                        scalar1=neg_mean_of[group][:, r : r + 1],
-                        scalar2=rstd_of[group][:, r : r + 1],
-                        op0=ALU.add,
-                        op1=ALU.mult,
-                    )
+                    u_half = u[:, r, half * CHANNELS : (half + 1) * CHANNELS]
+                    if r < SCALAR_TILES:
+                        nc.scalar.activation(
+                            out=u_half,
+                            in_=source,
+                            func=ACT.Identity,
+                            scale=rstd_of[group][:, r : r + 1],
+                            bias=shift_of[group][:, r : r + 1],
+                        )
+                    else:
+                        nc.gpsimd.tensor_scalar(
+                            out=u_half,
+                            in0=source,
+                            scalar1=neg_mean_of[group][:, r : r + 1],
+                            scalar2=rstd_of[group][:, r : r + 1],
+                            op0=ALU.add,
+                            op1=ALU.mult,
+                        )
             u_of[group] = u
 
         def transpose_and_scale(group):
@@ -264,12 +276,13 @@ def tile_textguidedcamfusion_pa_t_kernel(tc, pooled, proto, ln_g, ln_b, W, b, ou
             inv_norm = small.tile([P, TILES], F32)
             nc.vector.reciprocal(out=inv_norm[:], in_=norm_of[group][:])
             unit = o_pool.tile([P, TILES, D_OUT], F32)
-            out_rows = out[rows_of(group), :].rearrange("(p r) d -> p r d", r=TILES)
             for r in range(TILES):
                 nc.vector.tensor_scalar_mul(
                     out=unit[:, r, :], in0=relu_of[group][:, r, :], scalar1=inv_norm[:, r : r + 1]
                 )
-                nc.sync.dma_start(out=out_rows[:, r, :], in_=unit[:, r, :])
+            nc.sync.dma_start(
+                out=out[rows_of(group), :].rearrange("(p r) d -> p r d", r=TILES), in_=unit[:]
+            )
 
         def run(stage, group):
             if 0 <= group < GROUPS:
@@ -278,19 +291,15 @@ def tile_textguidedcamfusion_pa_t_kernel(tc, pooled, proto, ln_g, ln_b, W, b, ou
         with tc.manual_schedule():
             for step in range(-FIRST_STAGE_LEAD, GROUPS + LAST_STAGE_LAG):
                 run(load_rows, step + FIRST_STAGE_LEAD)
-                if step == WEIGHTS_LOAD_STEP:
-                    load_weights()
-                run(multiply, step - 2)
-                run(relu_and_squares, step - 3)
                 run(root_of_variance, step + 2)
                 run(root_of_squares, step - LAST_STAGE_LAG)
+                run(multiply, step - 2)
+                run(relu_and_squares, step - 3)
                 run(transpose_and_scale, step)
                 run(normalise, step + 1)
-                run(row_statistics, step + 3)
-                if step == WEIGHTS_QUANTISE_STEP:
-                    quantise_weights()
-                run(add_bias, step - 2)
                 run(quantise, step - 1)
+                run(add_bias, step - 2)
                 run(invert_std, step + 2)
                 run(floor_squares, step - 3)
                 run(store_unit_rows, step - LAST_STAGE_LAG)
+                run(row_statistics, step + 3)

@@ -164,29 +164,36 @@ def tile_textguidedcamfusion_pa_t_kernel(tc, pooled, proto, ln_g, ln_b, W, b, ou
             neg_mean_of[group] = neg_mean
             shift_of[group] = shift
 
-        def normalise(group):
+        def halves_of(group, r):
+            return [
+                (u_of[group][:, r, half * CHANNELS : (half + 1) * CHANNELS], source)
+                for half, source in ((0, x_of[group][:, r, :]), (1, context[:]))
+            ]
+
+        def normalise_on_gpsimd(group):
             u = u_pool.tile([P, TILES, FEATURES], F32)
-            for r in range(TILES):
-                for half, source in ((0, x_of[group][:, r, :]), (1, context[:])):
-                    u_half = u[:, r, half * CHANNELS : (half + 1) * CHANNELS]
-                    if r < SCALAR_TILES:
-                        nc.scalar.activation(
-                            out=u_half,
-                            in_=source,
-                            func=ACT.Identity,
-                            scale=rstd_of[group][:, r : r + 1],
-                            bias=shift_of[group][:, r : r + 1],
-                        )
-                    else:
-                        nc.gpsimd.tensor_scalar(
-                            out=u_half,
-                            in0=source,
-                            scalar1=neg_mean_of[group][:, r : r + 1],
-                            scalar2=rstd_of[group][:, r : r + 1],
-                            op0=ALU.add,
-                            op1=ALU.mult,
-                        )
             u_of[group] = u
+            for r in range(SCALAR_TILES, TILES):
+                for u_half, source in halves_of(group, r):
+                    nc.gpsimd.tensor_scalar(
+                        out=u_half,
+                        in0=source,
+                        scalar1=neg_mean_of[group][:, r : r + 1],
+                        scalar2=rstd_of[group][:, r : r + 1],
+                        op0=ALU.add,
+                        op1=ALU.mult,
+                    )
+
+        def normalise_on_scalar(group):
+            for r in range(SCALAR_TILES):
+                for u_half, source in halves_of(group, r):
+                    nc.scalar.activation(
+                        out=u_half,
+                        in_=source,
+                        func=ACT.Identity,
+                        scale=rstd_of[group][:, r : r + 1],
+                        bias=shift_of[group][:, r : r + 1],
+                    )
 
         def transpose_and_scale(group):
             z_planes = z_pool.tile([P, PASSES, PACK, GROUP_ROWS], BF16)
@@ -291,15 +298,16 @@ def tile_textguidedcamfusion_pa_t_kernel(tc, pooled, proto, ln_g, ln_b, W, b, ou
         with tc.manual_schedule():
             for step in range(-FIRST_STAGE_LEAD, GROUPS + LAST_STAGE_LAG):
                 run(load_rows, step + FIRST_STAGE_LEAD)
+                run(invert_std, step + 1)
+                run(normalise_on_gpsimd, step + 1)
+                run(row_statistics, step + 3)
                 run(root_of_variance, step + 2)
                 run(root_of_squares, step - LAST_STAGE_LAG)
                 run(multiply, step - 2)
+                run(add_bias, step - 2)
                 run(relu_and_squares, step - 3)
                 run(transpose_and_scale, step)
-                run(normalise, step + 1)
+                run(normalise_on_scalar, step + 1)
                 run(quantise, step - 1)
-                run(add_bias, step - 2)
-                run(invert_std, step + 2)
                 run(floor_squares, step - 3)
                 run(store_unit_rows, step - LAST_STAGE_LAG)
-                run(row_statistics, step + 3)

@@ -19,6 +19,7 @@ ROWS = 8192
 CHANNELS = 512
 FEATURES = 2 * CHANNELS
 D_OUT = 512
+D_BLOCKS = D_OUT // P
 PROTOS = 64
 PASSES = FEATURES // K_PASS
 BLOCKS = FEATURES // P
@@ -26,7 +27,6 @@ TILES = 4
 GROUP_ROWS = TILES * P
 GROUPS = ROWS // GROUP_ROWS
 STATS = 6
-SCALAR_TILES = 1
 LN_EPS = 1e-5
 NORM_FLOOR = 1e-12
 FIRST_STAGE_LEAD = 4
@@ -48,14 +48,15 @@ def tile_textguidedcamfusion_pa_t_kernel(tc, pooled, proto, ln_g, ln_b, W, b, ou
         const = stack.enter_context(tc.tile_pool(name="const", bufs=1))
         x_pool = stack.enter_context(tc.tile_pool(name="x", bufs=5))
         small = stack.enter_context(tc.tile_pool(name="small", bufs=4))
-        u_pool = stack.enter_context(tc.tile_pool(name="u", bufs=3))
+        u_pool = stack.enter_context(tc.tile_pool(name="u", bufs=2))
         z_pool = stack.enter_context(tc.tile_pool(name="z", bufs=2))
         q_pool = stack.enter_context(tc.tile_pool(name="q", bufs=3))
         h_pool = stack.enter_context(tc.tile_pool(name="h", bufs=2))
-        junk_pool = stack.enter_context(tc.tile_pool(name="junk", bufs=1))
+        junk_pool = stack.enter_context(tc.tile_pool(name="junk", bufs=2))
         o_pool = stack.enter_context(tc.tile_pool(name="o", bufs=2))
-        psum_t = stack.enter_context(tc.psum_pool(name="psum_t", bufs=4))
-        psum_acc = stack.enter_context(tc.psum_pool(name="psum_acc", bufs=4))
+        psum_t = stack.enter_context(tc.psum_pool(name="psum_t", bufs=2))
+        psum_acc = stack.enter_context(tc.psum_pool(name="psum_acc", bufs=2))
+        psum_back = stack.enter_context(tc.psum_pool(name="psum_back", bufs=4))
 
         identity = const.tile([P, P], F32)
         make_identity(nc, identity[:])
@@ -80,26 +81,22 @@ def tile_textguidedcamfusion_pa_t_kernel(tc, pooled, proto, ln_g, ln_b, W, b, ou
             in_=context_stats[:].unsqueeze(1).to_broadcast([P, GROUPS * TILES, STATS]),
         )
 
-        affine_rows = const.tile([P, P], BF16)
-        nc.vector.memset(affine_rows[:], 0.0)
-        nc.sync.dma_start(out=affine_rows[0:BLOCKS, :], in_=ln_g.rearrange("(q p) -> q p", p=P))
+        vector_rows = const.tile([P, P], BF16)
+        nc.vector.memset(vector_rows[:], 0.0)
+        nc.sync.dma_start(out=vector_rows[0:BLOCKS, :], in_=ln_g.rearrange("(q p) -> q p", p=P))
         nc.sync.dma_start(
-            out=affine_rows[BLOCKS : 2 * BLOCKS, :], in_=ln_b.rearrange("(q p) -> q p", p=P)
+            out=vector_rows[BLOCKS : 2 * BLOCKS, :], in_=ln_b.rearrange("(q p) -> q p", p=P)
         )
-        affine_rows_f32 = const.tile([P, P], F32)
-        nc.vector.tensor_copy(out=affine_rows_f32[:], in_=affine_rows[:])
-        affine_cols = psum_t.tile([P, P], F32, tag="ut")
-        nc.tensor.transpose(affine_cols[:], affine_rows_f32[:], identity[:])
-        gain_shift = const.tile([P, 2 * BLOCKS], F32)
-        nc.vector.tensor_copy(out=gain_shift[:], in_=affine_cols[:, 0 : 2 * BLOCKS])
-
-        bias_rows = const.tile([P, D_OUT], BF16)
-        nc.vector.memset(bias_rows[:], 0.0)
-        nc.sync.dma_start(out=bias_rows[0:1, :], in_=b.rearrange("(o d) -> o d", o=1))
-        bias_sum = psum_acc.tile([P, D_OUT], F32, tag="acc")
-        nc.tensor.matmul(bias_sum[:], lhsT=ones[:], rhs=bias_rows[:], start=True, stop=True)
-        bias = const.tile([P, D_OUT], F32)
-        nc.vector.tensor_copy(out=bias[:], in_=bias_sum[:])
+        nc.sync.dma_start(
+            out=vector_rows[2 * BLOCKS : 2 * BLOCKS + D_BLOCKS, :],
+            in_=b.rearrange("(q p) -> q p", p=P),
+        )
+        vector_rows_f32 = const.tile([P, P], F32)
+        nc.vector.tensor_copy(out=vector_rows_f32[:], in_=vector_rows[:])
+        vector_cols = psum_t.tile([P, P], F32, tag="ut")
+        nc.tensor.transpose(vector_cols[:], vector_rows_f32[:], identity[:])
+        per_partition = const.tile([P, 2 * BLOCKS + D_BLOCKS], F32)
+        nc.vector.tensor_copy(out=per_partition[:], in_=vector_cols[:, 0 : 2 * BLOCKS + D_BLOCKS])
 
         w_planes = const.tile([P, PASSES, PACK, D_OUT], BF16)
         nc.sync.dma_start(
@@ -118,8 +115,8 @@ def tile_textguidedcamfusion_pa_t_kernel(tc, pooled, proto, ln_g, ln_b, W, b, ou
             )
 
         x_of, mean_var_of, std_of, rstd_of, neg_mean_of, u_of = {}, {}, {}, {}, {}, {}
-        planes_of, codes_of, scales_of, acc_of, h_of, relu_of = {}, {}, {}, {}, {}, {}
-        sum_squares_of, floored_of, norm_of, shift_of = {}, {}, {}, {}
+        planes_of, codes_of, scales_of, relu_of, back_of = {}, {}, {}, {}, {}
+        sum_squares_of, norm_of, inv_norm_of, unit_of = {}, {}, {}, {}
 
         def rows_of(group):
             return slice(group * GROUP_ROWS, (group + 1) * GROUP_ROWS)
@@ -153,64 +150,51 @@ def tile_textguidedcamfusion_pa_t_kernel(tc, pooled, proto, ln_g, ln_b, W, b, ou
             rstd = small.tile([P, TILES], F32)
             nc.vector.reciprocal(out=rstd[:], in_=std_of[group][:])
             neg_mean = small.tile([P, TILES], F32)
-            nc.vector.tensor_scalar_mul(
-                out=neg_mean[:], in0=mean_var_of[group][:, :, 0], scalar1=-1.0
-            )
-            shift = small.tile([P, SCALAR_TILES], F32)
-            nc.vector.tensor_mul(
-                out=shift[:], in0=neg_mean[:, 0:SCALAR_TILES], in1=rstd[:, 0:SCALAR_TILES]
+            nc.gpsimd.tensor_scalar(
+                out=neg_mean[:],
+                in0=mean_var_of[group][:, :, 0],
+                scalar1=-1.0,
+                scalar2=0.0,
+                op0=ALU.mult,
+                op1=ALU.add,
             )
             rstd_of[group] = rstd
             neg_mean_of[group] = neg_mean
-            shift_of[group] = shift
 
-        def halves_of(group, r):
-            return [
-                (u_of[group][:, r, half * CHANNELS : (half + 1) * CHANNELS], source)
-                for half, source in ((0, x_of[group][:, r, :]), (1, context[:]))
-            ]
-
-        def normalise_on_gpsimd(group):
+        def normalise(group):
             u = u_pool.tile([P, TILES, FEATURES], F32)
-            u_of[group] = u
-            for r in range(SCALAR_TILES, TILES):
-                for u_half, source in halves_of(group, r):
+            for r in range(TILES):
+                for half, source in ((0, x_of[group][:, r, :]), (1, context[:])):
                     nc.gpsimd.tensor_scalar(
-                        out=u_half,
+                        out=u[:, r, half * CHANNELS : (half + 1) * CHANNELS],
                         in0=source,
                         scalar1=neg_mean_of[group][:, r : r + 1],
                         scalar2=rstd_of[group][:, r : r + 1],
                         op0=ALU.add,
                         op1=ALU.mult,
                     )
+            u_of[group] = u
 
-        def normalise_on_scalar(group):
-            for r in range(SCALAR_TILES):
-                for u_half, source in halves_of(group, r):
-                    nc.scalar.activation(
-                        out=u_half,
-                        in_=source,
-                        func=ACT.Identity,
-                        scale=rstd_of[group][:, r : r + 1],
-                        bias=shift_of[group][:, r : r + 1],
-                    )
-
-        def transpose_and_scale(group):
-            z_planes = z_pool.tile([P, PASSES, PACK, GROUP_ROWS], BF16)
-            for block in range(BLOCKS):
+        def transpose_and_scale(group, blocks):
+            if group not in planes_of:
+                z_planes = z_pool.tile([P, PASSES, PACK, GROUP_ROWS], BF16)
+                planes_of[group] = z_planes
+            banks = []
+            for block in blocks:
                 ut = psum_t.tile([P, TILES, P], F32, tag="ut")
                 for r in range(TILES):
                     nc.tensor.transpose(
                         ut[:, r, :], u_of[group][:, r, block * P : (block + 1) * P], identity[:]
                     )
+                banks.append(ut)
+            for block, ut in zip(blocks, banks):
                 nc.scalar.activation(
-                    out=z_planes[:, block // PACK, block % PACK, :],
+                    out=planes_of[group][:, block // PACK, block % PACK, :],
                     in_=ut[:].rearrange("p r i -> p (r i)"),
                     func=ACT.Identity,
-                    scale=gain_shift[:, block : block + 1],
-                    bias=gain_shift[:, BLOCKS + block : BLOCKS + block + 1],
+                    scale=per_partition[:, block : block + 1],
+                    bias=per_partition[:, BLOCKS + block : BLOCKS + block + 1],
                 )
-            planes_of[group] = z_planes
 
         def quantise(group):
             z_grouped = z_pool.tile([P, PASSES, GROUP_ROWS, PACK], BF16, align_bytes=64)
@@ -227,87 +211,92 @@ def tile_textguidedcamfusion_pa_t_kernel(tc, pooled, proto, ln_g, ln_b, W, b, ou
             codes_of[group] = z_codes
             scales_of[group] = z_scales
 
-        def multiply(group):
-            for r in range(TILES):
-                tile_cols = slice(r * P, (r + 1) * P)
-                acc = psum_acc.tile([P, D_OUT], F32, tag="acc")
+        def multiply_and_relu(group, d_blocks):
+            if group not in relu_of:
+                relu = h_pool.tile([P, D_BLOCKS, GROUP_ROWS], F32)
+                relu_of[group] = relu
+            banks = []
+            for d in d_blocks:
+                acc = psum_acc.tile([P, GROUP_ROWS], F32, tag="acc")
                 for g in range(PASSES):
                     nc.tensor.matmul_mx(
                         out=acc[:],
-                        lhsT=codes_of[group][:, g, tile_cols].bitcast(FP8X4),
-                        lhsT_scale=scales_of[group][:, g, tile_cols],
-                        rhs=w_codes[:, g, :].bitcast(FP8X4),
-                        rhs_scale=w_scales[:, g, :],
+                        lhsT=w_codes[:, g, d * P : (d + 1) * P].bitcast(FP8X4),
+                        lhsT_scale=w_scales[:, g, d * P : (d + 1) * P],
+                        rhs=codes_of[group][:, g, :].bitcast(FP8X4),
+                        rhs_scale=scales_of[group][:, g, :],
                         start=(g == 0),
                         stop=(g == PASSES - 1),
                     )
-                acc_of[group, r] = acc
-
-        def add_bias(group):
-            h = h_pool.tile([P, TILES, D_OUT], F32)
-            for r in range(TILES):
-                nc.vector.tensor_tensor(
-                    out=h[:, r, :], in0=acc_of[group, r][:], in1=bias[:], op=ALU.add
-                )
-            h_of[group] = h
-
-        def relu_and_squares(group):
-            relu = h_pool.tile([P, TILES, D_OUT], F32)
-            squares = junk_pool.tile([P, TILES, D_OUT], F32)
-            sum_squares = small.tile([P, TILES], F32)
-            for r in range(TILES):
-                nc.scalar.activation(out=relu[:, r, :], in_=h_of[group][:, r, :], func=ACT.Relu)
-            for r in range(TILES):
+                banks.append(acc)
+            for d, acc in zip(d_blocks, banks):
                 nc.scalar.activation(
-                    out=squares[:, r, :],
-                    in_=relu[:, r, :],
-                    func=ACT.Square,
-                    accum_out=sum_squares[:, r : r + 1],
+                    out=relu_of[group][:, d, :],
+                    in_=acc[:],
+                    func=ACT.Relu,
+                    bias=per_partition[:, 2 * BLOCKS + d : 2 * BLOCKS + d + 1],
                 )
-            relu_of[group] = relu
-            sum_squares_of[group] = sum_squares
 
-        def floor_squares(group):
-            floored = small.tile([P, TILES], F32)
-            nc.vector.tensor_scalar_max(
-                out=floored[:], in0=sum_squares_of[group][:], scalar1=NORM_FLOOR * NORM_FLOOR
-            )
-            floored_of[group] = floored
+        def rows_back_and_squares(group, tiles):
+            if group not in sum_squares_of:
+                sum_squares = small.tile([P, TILES], F32)
+                sum_squares_of[group] = sum_squares
+            for r in tiles:
+                back = psum_back.tile([P, D_BLOCKS, P], F32, tag="back")
+                for d in range(D_BLOCKS):
+                    nc.tensor.transpose(
+                        back[:, d, :], relu_of[group][:, d, r * P : (r + 1) * P], identity[:]
+                    )
+                back_of[group, r] = back
+            for r in tiles:
+                squares = junk_pool.tile([P, D_OUT], BF16)
+                nc.scalar.activation(
+                    out=squares[:],
+                    in_=back_of[group, r][:].rearrange("p d i -> p (d i)"),
+                    func=ACT.Square,
+                    accum_out=sum_squares_of[group][:, r : r + 1],
+                )
 
         def root_of_squares(group):
             norm = small.tile([P, TILES], F32)
-            nc.scalar.activation(out=norm[:], in_=floored_of[group][:], func=ACT.Sqrt)
+            nc.scalar.activation(out=norm[:], in_=sum_squares_of[group][:], func=ACT.Sqrt)
             norm_of[group] = norm
 
         def store_unit_rows(group):
+            floored = small.tile([P, TILES], F32)
+            nc.vector.tensor_scalar_max(out=floored[:], in0=norm_of[group][:], scalar1=NORM_FLOOR)
             inv_norm = small.tile([P, TILES], F32)
-            nc.vector.reciprocal(out=inv_norm[:], in_=norm_of[group][:])
+            nc.vector.reciprocal(out=inv_norm[:], in_=floored[:])
             unit = o_pool.tile([P, TILES, D_OUT], F32)
             for r in range(TILES):
                 nc.vector.tensor_scalar_mul(
-                    out=unit[:, r, :], in0=relu_of[group][:, r, :], scalar1=inv_norm[:, r : r + 1]
+                    out=unit[:, r, :],
+                    in0=back_of[group, r][:].rearrange("p d i -> p (d i)"),
+                    scalar1=inv_norm[:, r : r + 1],
                 )
             nc.sync.dma_start(
                 out=out[rows_of(group), :].rearrange("(p r) d -> p r d", r=TILES), in_=unit[:]
             )
 
-        def run(stage, group):
+        def run(stage, group, *parts):
             if 0 <= group < GROUPS:
-                stage(group)
+                stage(group, *parts)
 
         with tc.manual_schedule():
-            for step in range(-FIRST_STAGE_LEAD, GROUPS + LAST_STAGE_LAG):
+            for step in range(-FIRST_STAGE_LEAD, GROUPS + LAST_STAGE_LAG + 1):
                 run(load_rows, step + FIRST_STAGE_LEAD)
                 run(invert_std, step + 1)
-                run(normalise_on_gpsimd, step + 1)
-                run(row_statistics, step + 3)
-                run(root_of_variance, step + 2)
-                run(root_of_squares, step - LAST_STAGE_LAG)
-                run(multiply, step - 2)
-                run(add_bias, step - 2)
-                run(relu_and_squares, step - 3)
-                run(transpose_and_scale, step)
-                run(normalise_on_scalar, step + 1)
-                run(quantise, step - 1)
-                run(floor_squares, step - 3)
+                run(normalise, step + 1)
                 run(store_unit_rows, step - LAST_STAGE_LAG)
+                run(row_statistics, step + 3)
+                run(transpose_and_scale, step, (0, 1))
+                run(multiply_and_relu, step - 2, (0, 1))
+                run(transpose_and_scale, step, (2, 3))
+                run(multiply_and_relu, step - 2, (2, 3))
+                run(transpose_and_scale, step, (4, 5))
+                run(rows_back_and_squares, step - 3, (0, 1))
+                run(transpose_and_scale, step, (6, 7))
+                run(rows_back_and_squares, step - 3, (2, 3))
+                run(root_of_squares, step - 3)
+                run(root_of_variance, step + 2)
+                run(quantise, step - 1)

@@ -25,7 +25,12 @@ PASSES = FEATURES // K_PASS
 BLOCKS = FEATURES // P
 TILES = 4
 GROUP_ROWS = TILES * P
-GROUPS = ROWS // GROUP_ROWS
+GROUP_TILES = (1, 1, 2) + (TILES,) * 14 + (2, 1, 1)
+GROUPS = len(GROUP_TILES)
+FIRST_TILE = [sum(GROUP_TILES[:group]) for group in range(GROUPS)]
+ROW_TILES = ROWS // P
+assert sum(GROUP_TILES) == ROW_TILES
+GPSIMD_TILES = 3
 STATS = 6
 LN_EPS = 1e-5
 NORM_FLOOR = 1e-12
@@ -75,10 +80,10 @@ def tile_textguidedcamfusion_pa_t_kernel(tc, pooled, proto, ln_g, ln_b, W, b, ou
 
         context_stats = const.tile([P, STATS], F32)
         nc.vector.bn_stats(out=context_stats[:], in_=context[:])
-        stats = const.tile([P, GROUPS * TILES, 2, STATS], F32)
+        stats = const.tile([P, ROW_TILES, 2, STATS], F32)
         nc.vector.tensor_copy(
             out=stats[:, :, 1, :],
-            in_=context_stats[:].unsqueeze(1).to_broadcast([P, GROUPS * TILES, STATS]),
+            in_=context_stats[:].unsqueeze(1).to_broadcast([P, ROW_TILES, STATS]),
         )
 
         vector_rows = const.tile([P, P], BF16)
@@ -119,40 +124,49 @@ def tile_textguidedcamfusion_pa_t_kernel(tc, pooled, proto, ln_g, ln_b, W, b, ou
         sum_squares_of, norm_of, inv_norm_of, unit_of = {}, {}, {}, {}
 
         def rows_of(group):
-            return slice(group * GROUP_ROWS, (group + 1) * GROUP_ROWS)
+            return slice(FIRST_TILE[group] * P, (FIRST_TILE[group] + GROUP_TILES[group]) * P)
 
         def load_rows(group):
             x = x_pool.tile([P, TILES, CHANNELS], BF16)
+            tiles = GROUP_TILES[group]
             nc.sync.dma_start(
-                out=x[:], in_=pooled[rows_of(group), :].rearrange("(p r) k -> p r k", r=TILES)
+                out=x[:, 0:tiles, :],
+                in_=pooled[rows_of(group), :].rearrange("(p r) k -> p r k", r=tiles),
             )
             x_of[group] = x
 
         def row_statistics(group):
             mean_var = small.tile([P, TILES, 2], F32)
-            for r in range(TILES):
-                nc.vector.bn_stats(out=stats[:, group * TILES + r, 0, :], in_=x_of[group][:, r, :])
-            for r in range(TILES):
+            for r in range(GROUP_TILES[group]):
+                nc.vector.bn_stats(
+                    out=stats[:, FIRST_TILE[group] + r, 0, :], in_=x_of[group][:, r, :]
+                )
+            for r in range(GROUP_TILES[group]):
                 nc.vector.bn_aggr(
                     out=mean_var[:, r, :],
-                    in_=stats[:, group * TILES + r, :, :].rearrange("p a s -> p (a s)"),
+                    in_=stats[:, FIRST_TILE[group] + r, :, :].rearrange("p a s -> p (a s)"),
                 )
             mean_var_of[group] = mean_var
 
         def root_of_variance(group):
             std = small.tile([P, TILES], F32)
+            tiles = GROUP_TILES[group]
             nc.scalar.activation(
-                out=std[:], in_=mean_var_of[group][:, :, 1], func=ACT.Sqrt, bias=eps[:]
+                out=std[:, 0:tiles],
+                in_=mean_var_of[group][:, 0:tiles, 1],
+                func=ACT.Sqrt,
+                bias=eps[:],
             )
             std_of[group] = std
 
         def invert_std(group):
+            tiles = GROUP_TILES[group]
             rstd = small.tile([P, TILES], F32)
-            nc.vector.reciprocal(out=rstd[:], in_=std_of[group][:])
+            nc.vector.reciprocal(out=rstd[:, 0:tiles], in_=std_of[group][:, 0:tiles])
             neg_mean = small.tile([P, TILES], F32)
             nc.gpsimd.tensor_scalar(
-                out=neg_mean[:],
-                in0=mean_var_of[group][:, :, 0],
+                out=neg_mean[:, 0:tiles],
+                in0=mean_var_of[group][:, 0:tiles, 0],
                 scalar1=-1.0,
                 scalar2=0.0,
                 op0=ALU.mult,
@@ -161,36 +175,38 @@ def tile_textguidedcamfusion_pa_t_kernel(tc, pooled, proto, ln_g, ln_b, W, b, ou
             rstd_of[group] = rstd
             neg_mean_of[group] = neg_mean
 
-        def normalise(group):
-            u = u_pool.tile([P, TILES, FEATURES], F32)
-            for r in range(TILES):
+        def normalise(group, engine, tiles):
+            if group not in u_of:
+                u = u_pool.tile([P, TILES, FEATURES], F32)
+                u_of[group] = u
+            for r in [r for r in tiles if r < GROUP_TILES[group]]:
                 for half, source in ((0, x_of[group][:, r, :]), (1, context[:])):
-                    nc.gpsimd.tensor_scalar(
-                        out=u[:, r, half * CHANNELS : (half + 1) * CHANNELS],
+                    engine.tensor_scalar(
+                        out=u_of[group][:, r, half * CHANNELS : (half + 1) * CHANNELS],
                         in0=source,
                         scalar1=neg_mean_of[group][:, r : r + 1],
                         scalar2=rstd_of[group][:, r : r + 1],
                         op0=ALU.add,
                         op1=ALU.mult,
                     )
-            u_of[group] = u
 
         def transpose_and_scale(group, blocks):
             if group not in planes_of:
                 z_planes = z_pool.tile([P, PASSES, PACK, GROUP_ROWS], BF16)
                 planes_of[group] = z_planes
+            tiles = GROUP_TILES[group]
             banks = []
             for block in blocks:
                 ut = psum_t.tile([P, TILES, P], F32, tag="ut")
-                for r in range(TILES):
+                for r in range(tiles):
                     nc.tensor.transpose(
                         ut[:, r, :], u_of[group][:, r, block * P : (block + 1) * P], identity[:]
                     )
                 banks.append(ut)
             for block, ut in zip(blocks, banks):
                 nc.scalar.activation(
-                    out=planes_of[group][:, block // PACK, block % PACK, :],
-                    in_=ut[:].rearrange("p r i -> p (r i)"),
+                    out=planes_of[group][:, block // PACK, block % PACK, 0 : tiles * P],
+                    in_=ut[:, 0:tiles, :].rearrange("p r i -> p (r i)"),
                     func=ACT.Identity,
                     scale=per_partition[:, block : block + 1],
                     bias=per_partition[:, BLOCKS + block : BLOCKS + block + 1],
@@ -200,14 +216,22 @@ def tile_textguidedcamfusion_pa_t_kernel(tc, pooled, proto, ln_g, ln_b, W, b, ou
             z_grouped = z_pool.tile([P, PASSES, GROUP_ROWS, PACK], BF16, align_bytes=64)
             z_codes = q_pool.tile([P, PASSES, GROUP_ROWS], U32, align_bytes=64)
             z_scales = q_pool.tile([P, PASSES, GROUP_ROWS], U8, align_bytes=64)
+            rows = GROUP_TILES[group] * P
             for g in range(PASSES):
-                side_by_side(nc, z_grouped[:, g], planes_of[group][:, g])
-            for g in range(PASSES):
+                side_by_side(nc, z_grouped[:, g, 0:rows, :], planes_of[group][:, g, :, 0:rows])
+            if rows == GROUP_ROWS:
                 nc.vector.quantize_mx(
-                    out=z_codes[:, g, :].bitcast(FP8X4),
-                    scales=z_scales[:, g, :],
-                    in_=z_grouped[:, g].rearrange("p c t -> p (c t)"),
+                    out=z_codes[:].rearrange("p g c -> p (g c)").bitcast(FP8X4),
+                    scales=z_scales[:].rearrange("p g c -> p (g c)"),
+                    in_=z_grouped[:].rearrange("p g c t -> p (g c t)"),
                 )
+            else:
+                for g in range(PASSES):
+                    nc.vector.quantize_mx(
+                        out=z_codes[:, g, 0:rows].bitcast(FP8X4),
+                        scales=z_scales[:, g, 0:rows],
+                        in_=z_grouped[:, g, 0:rows, :].rearrange("p c t -> p (c t)"),
+                    )
             codes_of[group] = z_codes
             scales_of[group] = z_scales
 
@@ -215,24 +239,25 @@ def tile_textguidedcamfusion_pa_t_kernel(tc, pooled, proto, ln_g, ln_b, W, b, ou
             if group not in relu_of:
                 relu = h_pool.tile([P, D_BLOCKS, GROUP_ROWS], F32)
                 relu_of[group] = relu
+            rows = GROUP_TILES[group] * P
             banks = []
             for d in d_blocks:
                 acc = psum_acc.tile([P, GROUP_ROWS], F32, tag="acc")
                 for g in range(PASSES):
                     nc.tensor.matmul_mx(
-                        out=acc[:],
+                        out=acc[:, 0:rows],
                         lhsT=w_codes[:, g, d * P : (d + 1) * P].bitcast(FP8X4),
                         lhsT_scale=w_scales[:, g, d * P : (d + 1) * P],
-                        rhs=codes_of[group][:, g, :].bitcast(FP8X4),
-                        rhs_scale=scales_of[group][:, g, :],
+                        rhs=codes_of[group][:, g, 0:rows].bitcast(FP8X4),
+                        rhs_scale=scales_of[group][:, g, 0:rows],
                         start=(g == 0),
                         stop=(g == PASSES - 1),
                     )
                 banks.append(acc)
             for d, acc in zip(d_blocks, banks):
                 nc.scalar.activation(
-                    out=relu_of[group][:, d, :],
-                    in_=acc[:],
+                    out=relu_of[group][:, d, 0:rows],
+                    in_=acc[:, 0:rows],
                     func=ACT.Relu,
                     bias=per_partition[:, 2 * BLOCKS + d : 2 * BLOCKS + d + 1],
                 )
@@ -241,6 +266,7 @@ def tile_textguidedcamfusion_pa_t_kernel(tc, pooled, proto, ln_g, ln_b, W, b, ou
             if group not in sum_squares_of:
                 sum_squares = small.tile([P, TILES], F32)
                 sum_squares_of[group] = sum_squares
+            tiles = [r for r in tiles if r < GROUP_TILES[group]]
             for r in tiles:
                 back = psum_back.tile([P, D_BLOCKS, P], F32, tag="back")
                 for d in range(D_BLOCKS):
@@ -259,23 +285,30 @@ def tile_textguidedcamfusion_pa_t_kernel(tc, pooled, proto, ln_g, ln_b, W, b, ou
 
         def root_of_squares(group):
             norm = small.tile([P, TILES], F32)
-            nc.scalar.activation(out=norm[:], in_=sum_squares_of[group][:], func=ACT.Sqrt)
+            tiles = GROUP_TILES[group]
+            nc.scalar.activation(
+                out=norm[:, 0:tiles], in_=sum_squares_of[group][:, 0:tiles], func=ACT.Sqrt
+            )
             norm_of[group] = norm
 
         def store_unit_rows(group):
+            tiles = GROUP_TILES[group]
             floored = small.tile([P, TILES], F32)
-            nc.vector.tensor_scalar_max(out=floored[:], in0=norm_of[group][:], scalar1=NORM_FLOOR)
+            nc.vector.tensor_scalar_max(
+                out=floored[:, 0:tiles], in0=norm_of[group][:, 0:tiles], scalar1=NORM_FLOOR
+            )
             inv_norm = small.tile([P, TILES], F32)
-            nc.vector.reciprocal(out=inv_norm[:], in_=floored[:])
+            nc.vector.reciprocal(out=inv_norm[:, 0:tiles], in_=floored[:, 0:tiles])
             unit = o_pool.tile([P, TILES, D_OUT], F32)
-            for r in range(TILES):
+            for r in range(tiles):
                 nc.vector.tensor_scalar_mul(
                     out=unit[:, r, :],
                     in0=back_of[group, r][:].rearrange("p d i -> p (d i)"),
                     scalar1=inv_norm[:, r : r + 1],
                 )
             nc.sync.dma_start(
-                out=out[rows_of(group), :].rearrange("(p r) d -> p r d", r=TILES), in_=unit[:]
+                out=out[rows_of(group), :].rearrange("(p r) d -> p r d", r=tiles),
+                in_=unit[:, 0:tiles, :],
             )
 
         def run(stage, group, *parts):
@@ -286,17 +319,18 @@ def tile_textguidedcamfusion_pa_t_kernel(tc, pooled, proto, ln_g, ln_b, W, b, ou
             for step in range(-FIRST_STAGE_LEAD, GROUPS + LAST_STAGE_LAG + 1):
                 run(load_rows, step + FIRST_STAGE_LEAD)
                 run(invert_std, step + 1)
-                run(normalise, step + 1)
+                run(normalise, step + 1, nc.gpsimd, range(GPSIMD_TILES))
                 run(store_unit_rows, step - LAST_STAGE_LAG)
                 run(row_statistics, step + 3)
                 run(transpose_and_scale, step, (0, 1))
-                run(multiply_and_relu, step - 2, (0, 1))
                 run(transpose_and_scale, step, (2, 3))
-                run(multiply_and_relu, step - 2, (2, 3))
-                run(transpose_and_scale, step, (4, 5))
                 run(rows_back_and_squares, step - 3, (0, 1))
-                run(transpose_and_scale, step, (6, 7))
                 run(rows_back_and_squares, step - 3, (2, 3))
                 run(root_of_squares, step - 3)
                 run(root_of_variance, step + 2)
+                run(transpose_and_scale, step, (4, 5))
+                run(multiply_and_relu, step - 2, (0, 1))
+                run(transpose_and_scale, step, (6, 7))
+                run(multiply_and_relu, step - 2, (2, 3))
+                run(normalise, step + 1, nc.vector, range(GPSIMD_TILES, TILES))
                 run(quantise, step - 1)

@@ -320,17 +320,17 @@ def tile_textguidedcamfusion_pa_t_kernel(tc, pooled, proto, ln_g, ln_b, W, b, ou
                 run(load_rows, step + FIRST_STAGE_LEAD)
                 run(invert_std, step + 1)
                 run(normalise, step + 1, nc.gpsimd, range(GPSIMD_TILES))
-                run(store_unit_rows, step - LAST_STAGE_LAG)
                 run(row_statistics, step + 3)
+                run(store_unit_rows, step - LAST_STAGE_LAG)
                 run(transpose_and_scale, step, (0, 1))
+                run(multiply_and_relu, step - 2, (0, 1))
+                run(root_of_variance, step + 2)
                 run(transpose_and_scale, step, (2, 3))
+                run(multiply_and_relu, step - 2, (2, 3))
+                run(transpose_and_scale, step, (4, 5))
                 run(rows_back_and_squares, step - 3, (0, 1))
+                run(transpose_and_scale, step, (6, 7))
                 run(rows_back_and_squares, step - 3, (2, 3))
                 run(root_of_squares, step - 3)
-                run(root_of_variance, step + 2)
-                run(transpose_and_scale, step, (4, 5))
-                run(multiply_and_relu, step - 2, (0, 1))
-                run(transpose_and_scale, step, (6, 7))
-                run(multiply_and_relu, step - 2, (2, 3))
                 run(normalise, step + 1, nc.vector, range(GPSIMD_TILES, TILES))
                 run(quantise, step - 1)

@@ -121,7 +121,7 @@ def tile_textguidedcamfusion_pa_t_kernel(tc, pooled, proto, ln_g, ln_b, W, b, ou
 
         x_of, mean_var_of, std_of, rstd_of, neg_mean_of, u_of = {}, {}, {}, {}, {}, {}
         planes_of, codes_of, scales_of, relu_of, back_of = {}, {}, {}, {}, {}
-        sum_squares_of, norm_of, inv_norm_of, unit_of = {}, {}, {}, {}
+        sum_squares_of, norm_of, inv_norm_of, grouped_of = {}, {}, {}, {}
 
         def rows_of(group):
             return slice(FIRST_TILE[group] * P, (FIRST_TILE[group] + GROUP_TILES[group]) * P)
@@ -212,13 +212,18 @@ def tile_textguidedcamfusion_pa_t_kernel(tc, pooled, proto, ln_g, ln_b, W, b, ou
                     bias=per_partition[:, BLOCKS + block : BLOCKS + block + 1],
                 )
 
-        def quantise(group):
+        def group_words(group):
             z_grouped = z_pool.tile([P, PASSES, GROUP_ROWS, PACK], BF16, align_bytes=64)
-            z_codes = q_pool.tile([P, PASSES, GROUP_ROWS], U32, align_bytes=64)
-            z_scales = q_pool.tile([P, PASSES, GROUP_ROWS], U8, align_bytes=64)
             rows = GROUP_TILES[group] * P
             for g in range(PASSES):
                 side_by_side(nc, z_grouped[:, g, 0:rows, :], planes_of[group][:, g, :, 0:rows])
+            grouped_of[group] = z_grouped
+
+        def quantise(group):
+            z_grouped = grouped_of[group]
+            z_codes = q_pool.tile([P, PASSES, GROUP_ROWS], U32, align_bytes=64)
+            z_scales = q_pool.tile([P, PASSES, GROUP_ROWS], U8, align_bytes=64)
+            rows = GROUP_TILES[group] * P
             if rows == GROUP_ROWS:
                 nc.vector.quantize_mx(
                     out=z_codes[:].rearrange("p g c -> p (g c)").bitcast(FP8X4),
@@ -291,7 +296,7 @@ def tile_textguidedcamfusion_pa_t_kernel(tc, pooled, proto, ln_g, ln_b, W, b, ou
             )
             norm_of[group] = norm
 
-        def store_unit_rows(group):
+        def invert_norm(group):
             tiles = GROUP_TILES[group]
             floored = small.tile([P, TILES], F32)
             nc.vector.tensor_scalar_max(
@@ -299,6 +304,11 @@ def tile_textguidedcamfusion_pa_t_kernel(tc, pooled, proto, ln_g, ln_b, W, b, ou
             )
             inv_norm = small.tile([P, TILES], F32)
             nc.vector.reciprocal(out=inv_norm[:, 0:tiles], in_=floored[:, 0:tiles])
+            inv_norm_of[group] = inv_norm
+
+        def store_unit_rows(group):
+            tiles = GROUP_TILES[group]
+            inv_norm = inv_norm_of[group]
             unit = o_pool.tile([P, TILES, D_OUT], F32)
             for r in range(tiles):
                 nc.vector.tensor_scalar_mul(
@@ -320,17 +330,19 @@ def tile_textguidedcamfusion_pa_t_kernel(tc, pooled, proto, ln_g, ln_b, W, b, ou
                 run(load_rows, step + FIRST_STAGE_LEAD)
                 run(invert_std, step + 1)
                 run(normalise, step + 1, nc.gpsimd, range(GPSIMD_TILES))
-                run(row_statistics, step + 3)
                 run(store_unit_rows, step - LAST_STAGE_LAG)
+                run(row_statistics, step + 3)
                 run(transpose_and_scale, step, (0, 1))
-                run(multiply_and_relu, step - 2, (0, 1))
-                run(root_of_variance, step + 2)
-                run(transpose_and_scale, step, (2, 3))
-                run(multiply_and_relu, step - 2, (2, 3))
-                run(transpose_and_scale, step, (4, 5))
                 run(rows_back_and_squares, step - 3, (0, 1))
-                run(transpose_and_scale, step, (6, 7))
+                run(transpose_and_scale, step, (2, 3))
                 run(rows_back_and_squares, step - 3, (2, 3))
                 run(root_of_squares, step - 3)
+                run(root_of_variance, step + 2)
+                run(transpose_and_scale, step, (4, 5))
+                run(multiply_and_relu, step - 2, (0, 1))
+                run(transpose_and_scale, step, (6, 7))
+                run(multiply_and_relu, step - 2, (2, 3))
+                run(group_words, step - 1)
                 run(normalise, step + 1, nc.vector, range(GPSIMD_TILES, TILES))
+                run(invert_norm, step - 3)
                 run(quantise, step - 1)

@@ -37,6 +37,9 @@ NORM_FLOOR = 1e-12
 FIRST_STAGE_LEAD = 4
 LAST_STAGE_LAG = 4
 
+WEIGHTS_LOAD_STEP = -2
+WEIGHTS_QUANTISE_STEP = 0
+
 FLOPS = 2 * ROWS * FEATURES * D_OUT
 
 
@@ -71,7 +74,7 @@ def tile_textguidedcamfusion_pa_t_kernel(tc, pooled, proto, ln_g, ln_b, W, b, ou
         nc.vector.memset(eps[:], LN_EPS)
 
         proto_rows = const.tile([P, CHANNELS], BF16)
-        nc.vector.memset(proto_rows[:], 0.0)
+        nc.vector.memset(proto_rows[PROTOS:P, :], 0.0)
         nc.sync.dma_start(out=proto_rows[0:PROTOS, :], in_=proto)
         proto_sum = psum_acc.tile([P, CHANNELS], F32, tag="acc")
         nc.tensor.matmul(proto_sum[:], lhsT=ones[:], rhs=proto_rows[:], start=True, stop=True)
@@ -104,20 +107,24 @@ def tile_textguidedcamfusion_pa_t_kernel(tc, pooled, proto, ln_g, ln_b, W, b, ou
         nc.vector.tensor_copy(out=per_partition[:], in_=vector_cols[:, 0 : 2 * BLOCKS + D_BLOCKS])
 
         w_planes = const.tile([P, PASSES, PACK, D_OUT], BF16)
-        nc.sync.dma_start(
-            out=w_planes[:], in_=W.rearrange("(g t p) d -> p g t d", t=PACK, p=P)
-        )
         w_grouped = const.tile([P, PASSES, D_OUT, PACK], BF16, align_bytes=64)
         w_codes = const.tile([P, PASSES, D_OUT], U32, align_bytes=64)
         w_scales = const.tile([P, PASSES, D_OUT], U8, align_bytes=64)
-        for g in range(PASSES):
-            side_by_side(nc, w_grouped[:, g], w_planes[:, g])
-        for g in range(PASSES):
-            nc.vector.quantize_mx(
-                out=w_codes[:, g, :].bitcast(FP8X4),
-                scales=w_scales[:, g, :],
-                in_=w_grouped[:, g].rearrange("p d t -> p (d t)"),
+
+        def load_weights():
+            nc.sync.dma_start(
+                out=w_planes[:], in_=W.rearrange("(g t p) d -> p g t d", t=PACK, p=P)
             )
+
+        def quantise_weights():
+            for g in range(PASSES):
+                side_by_side(nc, w_grouped[:, g], w_planes[:, g])
+            for g in range(PASSES):
+                nc.vector.quantize_mx(
+                    out=w_codes[:, g, :].bitcast(FP8X4),
+                    scales=w_scales[:, g, :],
+                    in_=w_grouped[:, g].rearrange("p d t -> p (d t)"),
+                )
 
         x_of, mean_var_of, std_of, rstd_of, neg_mean_of, u_of = {}, {}, {}, {}, {}, {}
         planes_of, codes_of, scales_of, relu_of, back_of = {}, {}, {}, {}, {}
@@ -328,6 +335,8 @@ def tile_textguidedcamfusion_pa_t_kernel(tc, pooled, proto, ln_g, ln_b, W, b, ou
         with tc.manual_schedule():
             for step in range(-FIRST_STAGE_LEAD, GROUPS + LAST_STAGE_LAG + 1):
                 run(load_rows, step + FIRST_STAGE_LEAD)
+                if step == WEIGHTS_LOAD_STEP:
+                    load_weights()
                 run(invert_std, step + 1)
                 run(normalise, step + 1, nc.gpsimd, range(GPSIMD_TILES))
                 run(store_unit_rows, step - LAST_STAGE_LAG)
@@ -342,6 +351,8 @@ def tile_textguidedcamfusion_pa_t_kernel(tc, pooled, proto, ln_g, ln_b, W, b, ou
                 run(multiply_and_relu, step - 2, (0, 1))
                 run(transpose_and_scale, step, (6, 7))
                 run(multiply_and_relu, step - 2, (2, 3))
+                if step == WEIGHTS_QUANTISE_STEP:
+                    quantise_weights()
                 run(group_words, step - 1)
                 run(normalise, step + 1, nc.vector, range(GPSIMD_TILES, TILES))
                 run(invert_norm, step - 3)

@@ -30,7 +30,7 @@ GROUPS = len(GROUP_TILES)
 FIRST_TILE = [sum(GROUP_TILES[:group]) for group in range(GROUPS)]
 ROW_TILES = ROWS // P
 assert sum(GROUP_TILES) == ROW_TILES
-GPSIMD_TILES = 3
+GPSIMD_PIECES = 5
 STATS = 6
 LN_EPS = 1e-5
 NORM_FLOOR = 1e-12
@@ -182,12 +182,13 @@ def tile_textguidedcamfusion_pa_t_kernel(tc, pooled, proto, ln_g, ln_b, W, b, ou
             rstd_of[group] = rstd
             neg_mean_of[group] = neg_mean
 
-        def normalise(group, engine, tiles):
+        def normalise(group, engine, pieces):
             if group not in u_of:
                 u = u_pool.tile([P, TILES, FEATURES], F32)
                 u_of[group] = u
-            for r in [r for r in tiles if r < GROUP_TILES[group]]:
-                for half, source in ((0, x_of[group][:, r, :]), (1, context[:])):
+            for piece in [piece for piece in pieces if piece < 2 * GROUP_TILES[group]]:
+                r, half = divmod(piece, 2)
+                for source in (context[:] if half else x_of[group][:, r, :],):
                     engine.tensor_scalar(
                         out=u_of[group][:, r, half * CHANNELS : (half + 1) * CHANNELS],
                         in0=source,
@@ -338,7 +339,7 @@ def tile_textguidedcamfusion_pa_t_kernel(tc, pooled, proto, ln_g, ln_b, W, b, ou
                 if step == WEIGHTS_LOAD_STEP:
                     load_weights()
                 run(invert_std, step + 1)
-                run(normalise, step + 1, nc.gpsimd, range(GPSIMD_TILES))
+                run(normalise, step + 1, nc.gpsimd, range(GPSIMD_PIECES))
                 run(store_unit_rows, step - LAST_STAGE_LAG)
                 run(row_statistics, step + 3)
                 run(transpose_and_scale, step, (0, 1))
@@ -354,6 +355,6 @@ def tile_textguidedcamfusion_pa_t_kernel(tc, pooled, proto, ln_g, ln_b, W, b, ou
                 if step == WEIGHTS_QUANTISE_STEP:
                     quantise_weights()
                 run(group_words, step - 1)
-                run(normalise, step + 1, nc.vector, range(GPSIMD_TILES, TILES))
+                run(normalise, step + 1, nc.vector, range(GPSIMD_PIECES, 2 * TILES))
                 run(invert_norm, step - 3)
                 run(quantise, step - 1)

@@ -19,10 +19,10 @@ ROWS = 8192
 CHANNELS = 512
 FEATURES = 2 * CHANNELS
 D_OUT = 512
-D_BLOCKS = D_OUT // P
 PROTOS = 64
 PASSES = FEATURES // K_PASS
 BLOCKS = FEATURES // P
+HALF_BLOCKS = CHANNELS // P
 TILES = 4
 GROUP_ROWS = TILES * P
 GROUP_TILES = (1, 1, 2) + (TILES,) * 14 + (2, 1, 1)
@@ -30,12 +30,20 @@ GROUPS = len(GROUP_TILES)
 FIRST_TILE = [sum(GROUP_TILES[:group]) for group in range(GROUPS)]
 ROW_TILES = ROWS // P
 assert sum(GROUP_TILES) == ROW_TILES
+PRODUCT_GROUPS = range(5, 17)
 GPSIMD_PIECES = 5
+SCALAR_SQUARES = 2
 STATS = 6
 LN_EPS = 1e-5
 NORM_FLOOR = 1e-12
 FIRST_STAGE_LEAD = 4
 LAST_STAGE_LAG = 4
+
+QUADRANT = 32
+QUADRANTS = P // QUADRANT
+PARTS = 3
+SHIFT_QUADRANT = 3
+ONE_ROW = SHIFT_QUADRANT * QUADRANT + QUADRANT // 2
 
 WEIGHTS_LOAD_STEP = -2
 WEIGHTS_QUANTISE_STEP = 0
@@ -58,16 +66,19 @@ def tile_textguidedcamfusion_pa_t_kernel(tc, pooled, proto, ln_g, ln_b, W, b, ou
         small = stack.enter_context(tc.tile_pool(name="small", bufs=4))
         u_pool = stack.enter_context(tc.tile_pool(name="u", bufs=2))
         z_pool = stack.enter_context(tc.tile_pool(name="z", bufs=2))
+        grouped_pool = stack.enter_context(tc.tile_pool(name="grouped", bufs=3))
         q_pool = stack.enter_context(tc.tile_pool(name="q", bufs=3))
-        h_pool = stack.enter_context(tc.tile_pool(name="h", bufs=2))
+        h_pool = stack.enter_context(tc.tile_pool(name="h", bufs=3))
         junk_pool = stack.enter_context(tc.tile_pool(name="junk", bufs=2))
         o_pool = stack.enter_context(tc.tile_pool(name="o", bufs=2))
-        psum_t = stack.enter_context(tc.psum_pool(name="psum_t", bufs=2))
-        psum_acc = stack.enter_context(tc.psum_pool(name="psum_acc", bufs=2))
-        psum_back = stack.enter_context(tc.psum_pool(name="psum_back", bufs=4))
+        psum_u = stack.enter_context(tc.psum_pool(name="psum_u", bufs=2))
+        psum_c = stack.enter_context(tc.psum_pool(name="psum_c", bufs=2))
+        psum_acc = stack.enter_context(tc.psum_pool(name="psum_acc", bufs=4))
 
         identity = const.tile([P, P], F32)
         make_identity(nc, identity[:])
+        identity_bf16 = const.tile([P, P], BF16)
+        nc.gpsimd.tensor_copy(out=identity_bf16[:], in_=identity[:])
         ones = const.tile([P, P], BF16)
         nc.vector.memset(ones[:], 1.0)
         eps = const.tile([P, 1], F32)
@@ -95,16 +106,59 @@ def tile_textguidedcamfusion_pa_t_kernel(tc, pooled, proto, ln_g, ln_b, W, b, ou
         nc.sync.dma_start(
             out=vector_rows[BLOCKS : 2 * BLOCKS, :], in_=ln_b.rearrange("(q p) -> q p", p=P)
         )
-        nc.sync.dma_start(
-            out=vector_rows[2 * BLOCKS : 2 * BLOCKS + D_BLOCKS, :],
-            in_=b.rearrange("(q p) -> q p", p=P),
-        )
         vector_rows_f32 = const.tile([P, P], F32)
         nc.vector.tensor_copy(out=vector_rows_f32[:], in_=vector_rows[:])
-        vector_cols = psum_t.tile([P, P], F32, tag="ut")
+        vector_cols = psum_u.tile([P, P], F32, tag="ut")
         nc.tensor.transpose(vector_cols[:], vector_rows_f32[:], identity[:])
-        per_partition = const.tile([P, 2 * BLOCKS + D_BLOCKS], F32)
-        nc.vector.tensor_copy(out=per_partition[:], in_=vector_cols[:, 0 : 2 * BLOCKS + D_BLOCKS])
+        per_partition = const.tile([P, 2 * BLOCKS], F32)
+        nc.vector.tensor_copy(out=per_partition[:], in_=vector_cols[:, 0 : 2 * BLOCKS])
+
+        bias_rows = const.tile([P, D_OUT], BF16)
+        gain_rows = const.tile([P, CHANNELS], BF16)
+        features_side = const.tile([P, CHANNELS], BF16)
+        factor_tiles = [
+            const.tile([P, TILES, QUADRANTS, QUADRANT], BF16, name="factors_even"),
+            const.tile([P, TILES, QUADRANTS, QUADRANT], BF16, name="factors_odd"),
+        ]
+
+        def load_small_vectors():
+            nc.sync.dma_start(out=bias_rows[:], in_=b.partition_broadcast(P))
+            nc.sync.dma_start(
+                out=gain_rows[:], in_=ln_g[CHANNELS:FEATURES].partition_broadcast(P)
+            )
+            nc.sync.dma_start(
+                out=features_side[SHIFT_QUADRANT * QUADRANT : ONE_ROW, :],
+                in_=ln_g[CHANNELS:FEATURES].partition_broadcast(QUADRANT // 2),
+            )
+            nc.sync.dma_start(
+                out=features_side[ONE_ROW:P, :],
+                in_=ln_b[CHANNELS:FEATURES].partition_broadcast(QUADRANT // 2),
+            )
+
+        def clear_factors():
+            for factors in factor_tiles:
+                nc.gpsimd.memset(factors[:], 0.0)
+                nc.gpsimd.memset(factors[:, :, SHIFT_QUADRANT, QUADRANT // 2], 1.0)
+
+        rest_of = {}
+
+        def features_part(part):
+            if part == 0:
+                rest = const.tile([P, CHANNELS], F32, name="rest_0")
+                nc.vector.tensor_tensor(
+                    out=rest[:], in0=context[:], in1=gain_rows[:], op=ALU.mult
+                )
+            else:
+                rest = const.tile([P, CHANNELS], F32, name="rest_%d" % part)
+                nc.vector.tensor_tensor(
+                    out=rest[:], in0=rest_of[part - 1][0][:], in1=rest_of[part - 1][1][:],
+                    op=ALU.subtract,
+                )
+            rounded = const.tile([P, CHANNELS], BF16, name="rounded_%d" % part)
+            nc.vector.tensor_copy(out=rounded[:], in_=rest[:])
+            rows = slice(part * QUADRANT, (part + 1) * QUADRANT)
+            nc.vector.tensor_copy(out=features_side[rows, :], in_=rounded[rows, :])
+            rest_of[part] = (rest, rounded)
 
         w_planes = const.tile([P, PASSES, PACK, D_OUT], BF16)
         w_grouped = const.tile([P, PASSES, D_OUT, PACK], BF16, align_bytes=64)
@@ -126,12 +180,19 @@ def tile_textguidedcamfusion_pa_t_kernel(tc, pooled, proto, ln_g, ln_b, W, b, ou
                     in_=w_grouped[:, g].rearrange("p d t -> p (d t)"),
                 )
 
-        x_of, mean_var_of, std_of, rstd_of, neg_mean_of, u_of = {}, {}, {}, {}, {}, {}
-        planes_of, codes_of, scales_of, relu_of, back_of = {}, {}, {}, {}, {}
-        sum_squares_of, norm_of, inv_norm_of, grouped_of = {}, {}, {}, {}
+        x_of, mean_var_of, rstd_of, neg_mean_of, u_of = {}, {}, {}, {}, {}
+        factors_of, planes_of, codes_of, scales_of = {}, {}, {}, {}
+        acc_of, h_of, relu_of, unit_of = {}, {}, {}, {}
+        sum_squares_of, inv_norm_of, grouped_of = {}, {}, {}
 
         def rows_of(group):
             return slice(FIRST_TILE[group] * P, (FIRST_TILE[group] + GROUP_TILES[group]) * P)
+
+        def scalar_squares(group):
+            return SCALAR_SQUARES if GROUP_TILES[group] == TILES else 0
+
+        def vector_squares(group):
+            return GROUP_TILES[group] - scalar_squares(group)
 
         def load_rows(group):
             x = x_pool.tile([P, TILES, CHANNELS], BF16)
@@ -155,21 +216,19 @@ def tile_textguidedcamfusion_pa_t_kernel(tc, pooled, proto, ln_g, ln_b, W, b, ou
                 )
             mean_var_of[group] = mean_var
 
-        def root_of_variance(group):
-            std = small.tile([P, TILES], F32)
+        def inverse_std(group):
+            rstd = small.tile([P, TILES, QUADRANTS], F32)
             tiles = GROUP_TILES[group]
             nc.scalar.activation(
-                out=std[:, 0:tiles],
-                in_=mean_var_of[group][:, 0:tiles, 1],
-                func=ACT.Sqrt,
+                out=rstd[:, 0:tiles, 0:PARTS],
+                in_=mean_var_of[group][:, 0:tiles, 1].unsqueeze(2).to_broadcast([P, tiles, PARTS]),
+                func=ACT.Abs_reciprocal_sqrt,
                 bias=eps[:],
             )
-            std_of[group] = std
+            rstd_of[group] = rstd
 
-        def invert_std(group):
+        def negate_mean(group):
             tiles = GROUP_TILES[group]
-            rstd = small.tile([P, TILES], F32)
-            nc.vector.reciprocal(out=rstd[:, 0:tiles], in_=std_of[group][:, 0:tiles])
             neg_mean = small.tile([P, TILES], F32)
             nc.gpsimd.tensor_scalar(
                 out=neg_mean[:, 0:tiles],
@@ -179,39 +238,82 @@ def tile_textguidedcamfusion_pa_t_kernel(tc, pooled, proto, ln_g, ln_b, W, b, ou
                 op0=ALU.mult,
                 op1=ALU.add,
             )
-            rstd_of[group] = rstd
             neg_mean_of[group] = neg_mean
+
+        def row_factors(group):
+            if group not in PRODUCT_GROUPS:
+                return
+            rest = rstd_of[group]
+            nc.gpsimd.tensor_tensor(
+                out=rest[:, :, SHIFT_QUADRANT],
+                in0=neg_mean_of[group][:],
+                in1=rest[:, :, 0],
+                op=ALU.mult,
+            )
+            factors = factor_tiles[group % 2]
+            for part in range(PARTS):
+                nc.gpsimd.tensor_copy(out=factors[:, :, :, part], in_=rest[:])
+                if part < PARTS - 1:
+                    smaller = small.tile([P, TILES, QUADRANTS], F32)
+                    nc.gpsimd.tensor_tensor(
+                        out=smaller[:], in0=rest[:], in1=factors[:, :, :, part], op=ALU.subtract
+                    )
+                    rest = smaller
+
+        def transpose_factors(group):
+            if group not in PRODUCT_GROUPS:
+                return
+            turned = psum_c.tile([P, TILES, P], BF16, tag="ctx")
+            for r in range(TILES):
+                nc.tensor.transpose(
+                    turned[:, r, :],
+                    factor_tiles[group % 2][:, r].rearrange("p q i -> p (q i)"),
+                    identity_bf16[:],
+                )
+            factors = z_pool.tile([P, TILES, P], BF16)
+            nc.scalar.copy(
+                out=factors[:].rearrange("p r i -> p (r i)"),
+                in_=turned[:].rearrange("p r i -> p (r i)"),
+            )
+            factors_of[group] = factors
+
+        def pieces_of(group):
+            step = 2 if group in PRODUCT_GROUPS else 1
+            return list(range(0, 2 * GROUP_TILES[group], step))
 
         def normalise(group, engine, pieces):
             if group not in u_of:
                 u = u_pool.tile([P, TILES, FEATURES], F32)
                 u_of[group] = u
-            for piece in [piece for piece in pieces if piece < 2 * GROUP_TILES[group]]:
+            for piece in pieces:
                 r, half = divmod(piece, 2)
-                for source in (context[:] if half else x_of[group][:, r, :],):
-                    engine.tensor_scalar(
-                        out=u_of[group][:, r, half * CHANNELS : (half + 1) * CHANNELS],
-                        in0=source,
-                        scalar1=neg_mean_of[group][:, r : r + 1],
-                        scalar2=rstd_of[group][:, r : r + 1],
-                        op0=ALU.add,
-                        op1=ALU.mult,
-                    )
+                engine.tensor_scalar(
+                    out=u_of[group][:, r, half * CHANNELS : (half + 1) * CHANNELS],
+                    in0=context[:] if half else x_of[group][:, r, :],
+                    scalar1=neg_mean_of[group][:, r : r + 1],
+                    scalar2=rstd_of[group][:, r, 0:1],
+                    op0=ALU.add,
+                    op1=ALU.mult,
+                )
+
+        def normalise_gpsimd(group):
+            normalise(group, nc.gpsimd, [p for p in pieces_of(group) if p < GPSIMD_PIECES or group in PRODUCT_GROUPS])
+
+        def normalise_vector(group):
+            normalise(group, nc.vector, [p for p in pieces_of(group) if p >= GPSIMD_PIECES and group not in PRODUCT_GROUPS])
 
         def transpose_and_scale(group, blocks):
             if group not in planes_of:
                 z_planes = z_pool.tile([P, PASSES, PACK, GROUP_ROWS], BF16)
                 planes_of[group] = z_planes
             tiles = GROUP_TILES[group]
-            banks = []
             for block in blocks:
-                ut = psum_t.tile([P, TILES, P], F32, tag="ut")
+                pool, tag = (psum_c, "ctx") if block >= HALF_BLOCKS else (psum_u, "ut")
+                ut = pool.tile([P, TILES, P], F32, tag=tag, name="ut")
                 for r in range(tiles):
                     nc.tensor.transpose(
                         ut[:, r, :], u_of[group][:, r, block * P : (block + 1) * P], identity[:]
                     )
-                banks.append(ut)
-            for block, ut in zip(blocks, banks):
                 nc.scalar.activation(
                     out=planes_of[group][:, block // PACK, block % PACK, 0 : tiles * P],
                     in_=ut[:, 0:tiles, :].rearrange("p r i -> p (r i)"),
@@ -220,12 +322,37 @@ def tile_textguidedcamfusion_pa_t_kernel(tc, pooled, proto, ln_g, ln_b, W, b, ou
                     bias=per_partition[:, BLOCKS + block : BLOCKS + block + 1],
                 )
 
+        def grouped_tile(group):
+            if group not in grouped_of:
+                z_grouped = grouped_pool.tile([P, PASSES, GROUP_ROWS, PACK], BF16, align_bytes=64)
+                grouped_of[group] = z_grouped
+            return grouped_of[group]
+
+        def context_half(group, parts):
+            if group not in PRODUCT_GROUPS:
+                transpose_and_scale(group, [HALF_BLOCKS + part for part in parts])
+                return
+            z_grouped = grouped_tile(group)
+            for r in parts:
+                ctx = psum_c.tile([P, PACK, P], F32, tag="ctx")
+                for t in range(PACK):
+                    nc.tensor.matmul(
+                        ctx[:, t, :],
+                        lhsT=features_side[:, t * P : (t + 1) * P],
+                        rhs=factors_of[group][:, r, :],
+                        start=True,
+                        stop=True,
+                    )
+                nc.scalar.copy(
+                    out=z_grouped[:, 1, r * P : (r + 1) * P, :],
+                    in_=ctx[:].rearrange("p t i -> p i t"),
+                )
+
         def group_words(group):
-            z_grouped = z_pool.tile([P, PASSES, GROUP_ROWS, PACK], BF16, align_bytes=64)
+            z_grouped = grouped_tile(group)
             rows = GROUP_TILES[group] * P
-            for g in range(PASSES):
+            for g in range(1 if group in PRODUCT_GROUPS else PASSES):
                 side_by_side(nc, z_grouped[:, g, 0:rows, :], planes_of[group][:, g, :, 0:rows])
-            grouped_of[group] = z_grouped
 
         def quantise(group):
             z_grouped = grouped_of[group]
@@ -248,85 +375,117 @@ def tile_textguidedcamfusion_pa_t_kernel(tc, pooled, proto, ln_g, ln_b, W, b, ou
             codes_of[group] = z_codes
             scales_of[group] = z_scales
 
-        def multiply_and_relu(group, d_blocks):
-            if group not in relu_of:
-                relu = h_pool.tile([P, D_BLOCKS, GROUP_ROWS], F32)
-                relu_of[group] = relu
-            rows = GROUP_TILES[group] * P
-            banks = []
-            for d in d_blocks:
-                acc = psum_acc.tile([P, GROUP_ROWS], F32, tag="acc")
+        def multiply(group, tiles):
+            for r in tiles:
+                if r >= GROUP_TILES[group]:
+                    continue
+                acc = psum_acc.tile([P, D_OUT], F32, tag="acc")
                 for g in range(PASSES):
                     nc.tensor.matmul_mx(
-                        out=acc[:, 0:rows],
-                        lhsT=w_codes[:, g, d * P : (d + 1) * P].bitcast(FP8X4),
-                        lhsT_scale=w_scales[:, g, d * P : (d + 1) * P],
-                        rhs=codes_of[group][:, g, 0:rows].bitcast(FP8X4),
-                        rhs_scale=scales_of[group][:, g, 0:rows],
+                        out=acc[:],
+                        lhsT=codes_of[group][:, g, r * P : (r + 1) * P].bitcast(FP8X4),
+                        lhsT_scale=scales_of[group][:, g, r * P : (r + 1) * P],
+                        rhs=w_codes[:, g, :].bitcast(FP8X4),
+                        rhs_scale=w_scales[:, g, :],
                         start=(g == 0),
                         stop=(g == PASSES - 1),
                     )
-                banks.append(acc)
-            for d, acc in zip(d_blocks, banks):
-                nc.scalar.activation(
-                    out=relu_of[group][:, d, 0:rows],
-                    in_=acc[:, 0:rows],
-                    func=ACT.Relu,
-                    bias=per_partition[:, 2 * BLOCKS + d : 2 * BLOCKS + d + 1],
+                acc_of[group, r] = acc
+
+        def add_bias(group):
+            h = h_pool.tile([P, TILES, D_OUT], F32)
+            for r in range(GROUP_TILES[group]):
+                nc.vector.tensor_tensor(
+                    out=h[:, r, :], in0=acc_of[group, r][:], in1=bias_rows[:], op=ALU.add
+                )
+            h_of[group] = h
+            sum_squares = small.tile([P, TILES], F32)
+            sum_squares_of[group] = sum_squares
+
+        def squares_vector(group):
+            for r in range(vector_squares(group)):
+                squares = junk_pool.tile([P, D_OUT], BF16)
+                nc.vector.scalar_tensor_tensor(
+                    out=squares[:],
+                    in0=h_of[group][:, r, :],
+                    scalar=0.0,
+                    in1=h_of[group][:, r, :],
+                    op0=ALU.max,
+                    op1=ALU.mult,
+                    accum_out=sum_squares_of[group][:, r : r + 1],
                 )
 
-        def rows_back_and_squares(group, tiles):
-            if group not in sum_squares_of:
-                sum_squares = small.tile([P, TILES], F32)
-                sum_squares_of[group] = sum_squares
-            tiles = [r for r in tiles if r < GROUP_TILES[group]]
+        def squares_scalar(group):
+            tiles = range(vector_squares(group), GROUP_TILES[group])
+            if not tiles:
+                return
+            relu = h_pool.tile([P, SCALAR_SQUARES, D_OUT], F32)
+            relu_of[group] = relu
             for r in tiles:
-                back = psum_back.tile([P, D_BLOCKS, P], F32, tag="back")
-                for d in range(D_BLOCKS):
-                    nc.tensor.transpose(
-                        back[:, d, :], relu_of[group][:, d, r * P : (r + 1) * P], identity[:]
-                    )
-                back_of[group, r] = back
+                nc.scalar.activation(
+                    out=relu[:, r - tiles.start, :], in_=h_of[group][:, r, :], func=ACT.Relu
+                )
             for r in tiles:
-                squares = junk_pool.tile([P, D_OUT], BF16)
+                squares = junk_pool.tile([P, D_OUT], BF16, name="squares_scalar")
                 nc.scalar.activation(
                     out=squares[:],
-                    in_=back_of[group, r][:].rearrange("p d i -> p (d i)"),
+                    in_=relu[:, r - tiles.start, :],
                     func=ACT.Square,
                     accum_out=sum_squares_of[group][:, r : r + 1],
                 )
 
-        def root_of_squares(group):
-            norm = small.tile([P, TILES], F32)
-            tiles = GROUP_TILES[group]
-            nc.scalar.activation(
-                out=norm[:, 0:tiles], in_=sum_squares_of[group][:, 0:tiles], func=ACT.Sqrt
-            )
-            norm_of[group] = norm
-
-        def invert_norm(group):
+        def floor_of_squares(group):
             tiles = GROUP_TILES[group]
             floored = small.tile([P, TILES], F32)
-            nc.vector.tensor_scalar_max(
-                out=floored[:, 0:tiles], in0=norm_of[group][:, 0:tiles], scalar1=NORM_FLOOR
+            nc.gpsimd.tensor_scalar(
+                out=floored[:, 0:tiles],
+                in0=sum_squares_of[group][:, 0:tiles],
+                scalar1=NORM_FLOOR**2,
+                scalar2=0.0,
+                op0=ALU.max,
+                op1=ALU.add,
             )
+            sum_squares_of[group] = floored
+
+        def inverse_norm(group):
+            tiles = GROUP_TILES[group]
             inv_norm = small.tile([P, TILES], F32)
-            nc.vector.reciprocal(out=inv_norm[:, 0:tiles], in_=floored[:, 0:tiles])
+            nc.scalar.activation(
+                out=inv_norm[:, 0:tiles],
+                in_=sum_squares_of[group][:, 0:tiles],
+                func=ACT.Abs_reciprocal_sqrt,
+            )
             inv_norm_of[group] = inv_norm
+            unit = o_pool.tile([P, TILES, D_OUT], F32)
+            unit_of[group] = unit
+
+        def unit_rows_scalar(group):
+            for r in range(vector_squares(group)):
+                nc.scalar.activation(
+                    out=unit_of[group][:, r, :],
+                    in_=h_of[group][:, r, :],
+                    func=ACT.Relu,
+                    scale=inv_norm_of[group][:, r : r + 1],
+                )
+
+        def unit_rows_gpsimd(group):
+            engine = nc.gpsimd if group in PRODUCT_GROUPS else nc.vector
+            first = vector_squares(group)
+            for r in range(first, GROUP_TILES[group]):
+                engine.tensor_scalar(
+                    out=unit_of[group][:, r, :],
+                    in0=relu_of[group][:, r - first, :],
+                    scalar1=inv_norm_of[group][:, r : r + 1],
+                    scalar2=0.0,
+                    op0=ALU.mult,
+                    op1=ALU.add,
+                )
 
         def store_unit_rows(group):
             tiles = GROUP_TILES[group]
-            inv_norm = inv_norm_of[group]
-            unit = o_pool.tile([P, TILES, D_OUT], F32)
-            for r in range(tiles):
-                nc.vector.tensor_scalar_mul(
-                    out=unit[:, r, :],
-                    in0=back_of[group, r][:].rearrange("p d i -> p (d i)"),
-                    scalar1=inv_norm[:, r : r + 1],
-                )
             nc.sync.dma_start(
                 out=out[rows_of(group), :].rearrange("(p r) d -> p r d", r=tiles),
-                in_=unit[:, 0:tiles, :],
+                in_=unit_of[group][:, 0:tiles, :],
             )
 
         def run(stage, group, *parts):
@@ -338,23 +497,34 @@ def tile_textguidedcamfusion_pa_t_kernel(tc, pooled, proto, ln_g, ln_b, W, b, ou
                 run(load_rows, step + FIRST_STAGE_LEAD)
                 if step == WEIGHTS_LOAD_STEP:
                     load_weights()
-                run(invert_std, step + 1)
-                run(normalise, step + 1, nc.gpsimd, range(GPSIMD_PIECES))
-                run(store_unit_rows, step - LAST_STAGE_LAG)
-                run(row_statistics, step + 3)
+                if step == WEIGHTS_LOAD_STEP + 1:
+                    load_small_vectors()
+                run(negate_mean, step + 1)
+                run(row_factors, step + 1)
+                run(normalise_gpsimd, step + 1)
+                run(inverse_norm, step - 4)
+                run(add_bias, step - 3)
+                run(row_statistics, step + 2)
                 run(transpose_and_scale, step, (0, 1))
-                run(rows_back_and_squares, step - 3, (0, 1))
+                run(context_half, step, (0, 1))
+                run(unit_rows_scalar, step - 4)
+                run(multiply, step - 2, (0, 1))
+                run(squares_scalar, step - 3)
                 run(transpose_and_scale, step, (2, 3))
-                run(rows_back_and_squares, step - 3, (2, 3))
-                run(root_of_squares, step - 3)
-                run(root_of_variance, step + 2)
-                run(transpose_and_scale, step, (4, 5))
-                run(multiply_and_relu, step - 2, (0, 1))
-                run(transpose_and_scale, step, (6, 7))
-                run(multiply_and_relu, step - 2, (2, 3))
+                run(context_half, step, (2, 3))
+                run(multiply, step - 2, (2, 3))
                 if step == WEIGHTS_QUANTISE_STEP:
                     quantise_weights()
+                if step == 0:
+                    clear_factors()
                 run(group_words, step - 1)
-                run(normalise, step + 1, nc.vector, range(GPSIMD_PIECES, 2 * TILES))
-                run(invert_norm, step - 3)
+                run(unit_rows_gpsimd, step - 4)
+                run(store_unit_rows, step - 4)
+                run(squares_vector, step - 3)
+                run(normalise_vector, step + 1)
+                if 1 <= step <= PARTS:
+                    features_part(step - 1)
+                run(floor_of_squares, step - 3)
                 run(quantise, step - 1)
+                run(inverse_std, step + 2)
+                run(transpose_factors, step + 1)

@@ -230,13 +230,8 @@ def tile_textguidedcamfusion_pa_t_kernel(tc, pooled, proto, ln_g, ln_b, W, b, ou
         def negate_mean(group):
             tiles = GROUP_TILES[group]
             neg_mean = small.tile([P, TILES], F32)
-            nc.gpsimd.tensor_scalar(
-                out=neg_mean[:, 0:tiles],
-                in0=mean_var_of[group][:, 0:tiles, 0],
-                scalar1=-1.0,
-                scalar2=0.0,
-                op0=ALU.mult,
-                op1=ALU.add,
+            nc.vector.tensor_scalar_mul(
+                out=neg_mean[:, 0:tiles], in0=mean_var_of[group][:, 0:tiles, 0], scalar1=-1.0
             )
             neg_mean_of[group] = neg_mean
 
@@ -437,13 +432,10 @@ def tile_textguidedcamfusion_pa_t_kernel(tc, pooled, proto, ln_g, ln_b, W, b, ou
         def floor_of_squares(group):
             tiles = GROUP_TILES[group]
             floored = small.tile([P, TILES], F32)
-            nc.gpsimd.tensor_scalar(
+            nc.vector.tensor_scalar_max(
                 out=floored[:, 0:tiles],
                 in0=sum_squares_of[group][:, 0:tiles],
                 scalar1=NORM_FLOOR**2,
-                scalar2=0.0,
-                op0=ALU.max,
-                op1=ALU.add,
             )
             sum_squares_of[group] = floored
 
@@ -468,11 +460,10 @@ def tile_textguidedcamfusion_pa_t_kernel(tc, pooled, proto, ln_g, ln_b, W, b, ou
                     scale=inv_norm_of[group][:, r : r + 1],
                 )
 
-        def unit_rows_gpsimd(group):
-            engine = nc.gpsimd if group in PRODUCT_GROUPS else nc.vector
+        def unit_rows_vector(group):
             first = vector_squares(group)
             for r in range(first, GROUP_TILES[group]):
-                engine.tensor_scalar(
+                nc.vector.tensor_scalar(
                     out=unit_of[group][:, r, :],
                     in0=relu_of[group][:, r - first, :],
                     scalar1=inv_norm_of[group][:, r : r + 1],
@@ -499,9 +490,10 @@ def tile_textguidedcamfusion_pa_t_kernel(tc, pooled, proto, ln_g, ln_b, W, b, ou
                     load_weights()
                 if step == WEIGHTS_LOAD_STEP + 1:
                     load_small_vectors()
+                run(floor_of_squares, step - 4)
                 run(negate_mean, step + 1)
-                run(row_factors, step + 1)
                 run(normalise_gpsimd, step + 1)
+                run(row_factors, step + 1)
                 run(inverse_norm, step - 4)
                 run(add_bias, step - 3)
                 run(row_statistics, step + 2)
@@ -518,13 +510,12 @@ def tile_textguidedcamfusion_pa_t_kernel(tc, pooled, proto, ln_g, ln_b, W, b, ou
                 if step == 0:
                     clear_factors()
                 run(group_words, step - 1)
-                run(unit_rows_gpsimd, step - 4)
+                run(unit_rows_vector, step - 4)
                 run(store_unit_rows, step - 4)
                 run(squares_vector, step - 3)
                 run(normalise_vector, step + 1)
                 if 1 <= step <= PARTS:
                     features_part(step - 1)
-                run(floor_of_squares, step - 3)
                 run(quantise, step - 1)
                 run(inverse_std, step + 2)
                 run(transpose_factors, step + 1)

@@ -292,10 +292,10 @@ def tile_textguidedcamfusion_pa_t_kernel(tc, pooled, proto, ln_g, ln_b, W, b, ou
                 )
 
         def normalise_gpsimd(group):
-            normalise(group, nc.gpsimd, [p for p in pieces_of(group) if p < GPSIMD_PIECES or group in PRODUCT_GROUPS])
+            normalise(group, nc.gpsimd, [piece for piece in pieces_of(group) if piece < GPSIMD_PIECES])
 
         def normalise_vector(group):
-            normalise(group, nc.vector, [p for p in pieces_of(group) if p >= GPSIMD_PIECES and group not in PRODUCT_GROUPS])
+            normalise(group, nc.vector, [piece for piece in pieces_of(group) if piece >= GPSIMD_PIECES])
 
         def transpose_and_scale(group, blocks):
             if group not in planes_of:

@@ -182,7 +182,7 @@ def tile_textguidedcamfusion_pa_t_kernel(tc, pooled, proto, ln_g, ln_b, W, b, ou
 
         x_of, mean_var_of, rstd_of, neg_mean_of, u_of = {}, {}, {}, {}, {}
         factors_of, planes_of, codes_of, scales_of = {}, {}, {}, {}
-        acc_of, h_of, relu_of, unit_of = {}, {}, {}, {}
+        acc_of, h_of, unit_of = {}, {}, {}
         sum_squares_of, inv_norm_of, grouped_of = {}, {}, {}
 
         def rows_of(group):
@@ -414,8 +414,7 @@ def tile_textguidedcamfusion_pa_t_kernel(tc, pooled, proto, ln_g, ln_b, W, b, ou
             tiles = range(vector_squares(group), GROUP_TILES[group])
             if not tiles:
                 return
-            relu = h_pool.tile([P, SCALAR_SQUARES, D_OUT], F32)
-            relu_of[group] = relu
+            relu = junk_pool.tile([P, SCALAR_SQUARES, D_OUT], F32)
             for r in tiles:
                 nc.scalar.activation(
                     out=relu[:, r - tiles.start, :], in_=h_of[group][:, r, :], func=ACT.Relu
@@ -451,25 +450,13 @@ def tile_textguidedcamfusion_pa_t_kernel(tc, pooled, proto, ln_g, ln_b, W, b, ou
             unit = o_pool.tile([P, TILES, D_OUT], F32)
             unit_of[group] = unit
 
-        def unit_rows_scalar(group):
-            for r in range(vector_squares(group)):
+        def unit_rows(group, tiles):
+            for r in [r for r in tiles if r < GROUP_TILES[group]]:
                 nc.scalar.activation(
                     out=unit_of[group][:, r, :],
                     in_=h_of[group][:, r, :],
                     func=ACT.Relu,
                     scale=inv_norm_of[group][:, r : r + 1],
-                )
-
-        def unit_rows_vector(group):
-            first = vector_squares(group)
-            for r in range(first, GROUP_TILES[group]):
-                nc.vector.tensor_scalar(
-                    out=unit_of[group][:, r, :],
-                    in0=relu_of[group][:, r - first, :],
-                    scalar1=inv_norm_of[group][:, r : r + 1],
-                    scalar2=0.0,
-                    op0=ALU.mult,
-                    op1=ALU.add,
                 )
 
         def store_unit_rows(group):
@@ -498,24 +485,26 @@ def tile_textguidedcamfusion_pa_t_kernel(tc, pooled, proto, ln_g, ln_b, W, b, ou
                 run(add_bias, step - 3)
                 run(row_statistics, step + 2)
                 run(transpose_and_scale, step, (0, 1))
+                run(unit_rows, step - 4, (0, 1))
+                run(multiply, step - 2, (0,))
                 run(context_half, step, (0, 1))
-                run(unit_rows_scalar, step - 4)
-                run(multiply, step - 2, (0, 1))
+                run(multiply, step - 2, (1,))
                 run(squares_scalar, step - 3)
                 run(transpose_and_scale, step, (2, 3))
+                run(inverse_std, step + 2)
+                run(unit_rows, step - 4, (2, 3))
+                run(store_unit_rows, step - 4)
+                run(multiply, step - 2, (2,))
                 run(context_half, step, (2, 3))
-                run(multiply, step - 2, (2, 3))
+                run(multiply, step - 2, (3,))
                 if step == WEIGHTS_QUANTISE_STEP:
                     quantise_weights()
                 if step == 0:
                     clear_factors()
                 run(group_words, step - 1)
-                run(unit_rows_vector, step - 4)
-                run(store_unit_rows, step - 4)
-                run(squares_vector, step - 3)
                 run(normalise_vector, step + 1)
+                run(squares_vector, step - 3)
                 if 1 <= step <= PARTS:
                     features_part(step - 1)
                 run(quantise, step - 1)
-                run(inverse_std, step + 2)
                 run(transpose_factors, step + 1)

@@ -25,12 +25,25 @@ BLOCKS = FEATURES // P
 HALF_BLOCKS = CHANNELS // P
 TILES = 4
 GROUP_ROWS = TILES * P
-GROUP_TILES = (1, 1, 2) + (TILES,) * 14 + (2, 1, 1)
+GROUP_TILES = (2,) + (TILES,) * 15 + (2,)
 GROUPS = len(GROUP_TILES)
 FIRST_TILE = [sum(GROUP_TILES[:group]) for group in range(GROUPS)]
 ROW_TILES = ROWS // P
+FIRST_FULL = 3
 assert sum(GROUP_TILES) == ROW_TILES
-PRODUCT_GROUPS = range(5, 17)
+PRODUCT_GROUPS = range(4, 17)
+LQ = 1
+LM = 2
+LA = 3
+LC = 4
+A_FIRST = True
+Y_EARLY = True
+MXPOS = (0, 1, 2, 3)
+GPIECES = {0: 0}
+SQ_FULL = "VVSS"
+UN_FULL = "VSSG"
+SQ = {0: "SS", GROUPS - 1: "VV"}
+UN = {0: "SS", GROUPS - 1: "VS"}
 GPSIMD_PIECES = 5
 SCALAR_SQUARES = 2
 STATS = 6
@@ -51,8 +64,8 @@ WEIGHTS_QUANTISE_STEP = 0
 FLOPS = 2 * ROWS * FEATURES * D_OUT
 
 
-def side_by_side(nc, grouped, planes):
-    nc.vector.tensor_copy(
+def side_by_side(copy, grouped, planes):
+    copy(
         out=grouped.rearrange("p (c i) t -> p c t i", i=4),
         in_=planes.rearrange("p t (c i) -> p c t i", i=4),
     )
@@ -75,18 +88,54 @@ def tile_textguidedcamfusion_pa_t_kernel(tc, pooled, proto, ln_g, ln_b, W, b, ou
         psum_c = stack.enter_context(tc.psum_pool(name="psum_c", bufs=2))
         psum_acc = stack.enter_context(tc.psum_pool(name="psum_acc", bufs=4))
 
+        stack.enter_context(tc.manual_schedule())
+        x_of = {}
+
+        def rows_of(group):
+            return slice(FIRST_TILE[group] * P, (FIRST_TILE[group] + GROUP_TILES[group]) * P)
+
+        def load_rows(group):
+            x = x_pool.tile([P, TILES, CHANNELS], BF16)
+            tiles = GROUP_TILES[group]
+            nc.sync.dma_start(
+                out=x[:, 0:tiles, :],
+                in_=pooled[rows_of(group), :].rearrange("(p r) k -> p r k", r=tiles),
+            )
+            x_of[group] = x
+
+        ones = const.tile([P, P], BF16)
+        nc.vector.memset(ones[:], 1.0)
+        proto_rows = const.tile([P, CHANNELS], BF16)
+        nc.vector.memset(proto_rows[PROTOS:P, :], 0.0)
+        vector_rows = const.tile([P, P], BF16)
+        nc.vector.memset(vector_rows[:], 0.0)
+        eps = const.tile([P, 1], F32)
+        nc.vector.memset(eps[:], LN_EPS)
+        floor = const.tile([P, 2], F32)
+        nc.vector.memset(floor[:, 0:1], -(NORM_FLOOR**2))
+        nc.vector.memset(floor[:, 1:2], NORM_FLOOR**2)
         identity = const.tile([P, P], F32)
         make_identity(nc, identity[:])
         identity_bf16 = const.tile([P, P], BF16)
         nc.gpsimd.tensor_copy(out=identity_bf16[:], in_=identity[:])
-        ones = const.tile([P, P], BF16)
-        nc.vector.memset(ones[:], 1.0)
-        eps = const.tile([P, 1], F32)
-        nc.vector.memset(eps[:], LN_EPS)
 
-        proto_rows = const.tile([P, CHANNELS], BF16)
-        nc.vector.memset(proto_rows[PROTOS:P, :], 0.0)
+        load_rows(0)
         nc.sync.dma_start(out=proto_rows[0:PROTOS, :], in_=proto)
+        nc.sync.dma_start(out=vector_rows[0:BLOCKS, :], in_=ln_g.rearrange("(q p) -> q p", p=P))
+        nc.sync.dma_start(
+            out=vector_rows[BLOCKS : 2 * BLOCKS, :], in_=ln_b.rearrange("(q p) -> q p", p=P)
+        )
+
+        stats = const.tile([P, ROW_TILES, 2, STATS], F32)
+
+        def own_statistics(group):
+            for r in range(GROUP_TILES[group]):
+                nc.vector.bn_stats(
+                    out=stats[:, FIRST_TILE[group] + r, 0, :], in_=x_of[group][:, r, :]
+                )
+
+        own_statistics(0)
+
         proto_sum = psum_acc.tile([P, CHANNELS], F32, tag="acc")
         nc.tensor.matmul(proto_sum[:], lhsT=ones[:], rhs=proto_rows[:], start=True, stop=True)
         context = const.tile([P, CHANNELS], F32)
@@ -94,24 +143,17 @@ def tile_textguidedcamfusion_pa_t_kernel(tc, pooled, proto, ln_g, ln_b, W, b, ou
 
         context_stats = const.tile([P, STATS], F32)
         nc.vector.bn_stats(out=context_stats[:], in_=context[:])
-        stats = const.tile([P, ROW_TILES, 2, STATS], F32)
         nc.vector.tensor_copy(
             out=stats[:, :, 1, :],
             in_=context_stats[:].unsqueeze(1).to_broadcast([P, ROW_TILES, STATS]),
         )
 
-        vector_rows = const.tile([P, P], BF16)
-        nc.vector.memset(vector_rows[:], 0.0)
-        nc.sync.dma_start(out=vector_rows[0:BLOCKS, :], in_=ln_g.rearrange("(q p) -> q p", p=P))
-        nc.sync.dma_start(
-            out=vector_rows[BLOCKS : 2 * BLOCKS, :], in_=ln_b.rearrange("(q p) -> q p", p=P)
-        )
         vector_rows_f32 = const.tile([P, P], F32)
-        nc.vector.tensor_copy(out=vector_rows_f32[:], in_=vector_rows[:])
+        nc.scalar.copy(out=vector_rows_f32[:], in_=vector_rows[:])
         vector_cols = psum_u.tile([P, P], F32, tag="ut")
         nc.tensor.transpose(vector_cols[:], vector_rows_f32[:], identity[:])
         per_partition = const.tile([P, 2 * BLOCKS], F32)
-        nc.vector.tensor_copy(out=per_partition[:], in_=vector_cols[:, 0 : 2 * BLOCKS])
+        nc.scalar.copy(out=per_partition[:], in_=vector_cols[:, 0 : 2 * BLOCKS])
 
         bias_rows = const.tile([P, D_OUT], BF16)
         gain_rows = const.tile([P, CHANNELS], BF16)
@@ -142,23 +184,29 @@ def tile_textguidedcamfusion_pa_t_kernel(tc, pooled, proto, ln_g, ln_b, W, b, ou
 
         rest_of = {}
 
-        def features_part(part):
+        def features_rest(part):
+            rest = const.tile([P, CHANNELS], F32, name="rest_%d" % part)
             if part == 0:
-                rest = const.tile([P, CHANNELS], F32, name="rest_0")
                 nc.vector.tensor_tensor(
                     out=rest[:], in0=context[:], in1=gain_rows[:], op=ALU.mult
                 )
             else:
-                rest = const.tile([P, CHANNELS], F32, name="rest_%d" % part)
+                before, rounded = rest_of[part - 1]
                 nc.vector.tensor_tensor(
-                    out=rest[:], in0=rest_of[part - 1][0][:], in1=rest_of[part - 1][1][:],
-                    op=ALU.subtract,
+                    out=rest[:], in0=before[:], in1=rounded[:], op=ALU.subtract
                 )
-            rounded = const.tile([P, CHANNELS], BF16, name="rounded_%d" % part)
-            nc.vector.tensor_copy(out=rounded[:], in_=rest[:])
+            rest_of[part] = rest
+
+        def features_round(part):
+            rest = rest_of[part]
             rows = slice(part * QUADRANT, (part + 1) * QUADRANT)
-            nc.vector.tensor_copy(out=features_side[rows, :], in_=rounded[rows, :])
-            rest_of[part] = (rest, rounded)
+            nc.scalar.copy(out=features_side[rows, :], in_=rest[rows, :])
+            if part < PARTS - 1:
+                rounded = const.tile([P, CHANNELS], BF16, name="rounded_%d" % part)
+                nc.scalar.copy(out=rounded[:], in_=rest[:])
+                rest_of[part] = (rest, rounded)
+
+        clear_factors()
 
         w_planes = const.tile([P, PASSES, PACK, D_OUT], BF16)
         w_grouped = const.tile([P, PASSES, D_OUT, PACK], BF16, align_bytes=64)
@@ -170,45 +218,29 @@ def tile_textguidedcamfusion_pa_t_kernel(tc, pooled, proto, ln_g, ln_b, W, b, ou
                 out=w_planes[:], in_=W.rearrange("(g t p) d -> p g t d", t=PACK, p=P)
             )
 
-        def quantise_weights():
-            for g in range(PASSES):
-                side_by_side(nc, w_grouped[:, g], w_planes[:, g])
-            for g in range(PASSES):
-                nc.vector.quantize_mx(
-                    out=w_codes[:, g, :].bitcast(FP8X4),
-                    scales=w_scales[:, g, :],
-                    in_=w_grouped[:, g].rearrange("p d t -> p (d t)"),
-                )
+        def weight_words(g):
+            side_by_side(nc.scalar.copy, w_grouped[:, g], w_planes[:, g])
 
-        x_of, mean_var_of, rstd_of, neg_mean_of, u_of = {}, {}, {}, {}, {}
-        factors_of, planes_of, codes_of, scales_of = {}, {}, {}, {}
-        acc_of, h_of, unit_of = {}, {}, {}
+        def quantise_weights(g):
+            nc.vector.quantize_mx(
+                out=w_codes[:, g, :].bitcast(FP8X4),
+                scales=w_scales[:, g, :],
+                in_=w_grouped[:, g].rearrange("p d t -> p (d t)"),
+            )
+
+        mean_var_of, rstd_of, neg_mean_of, u_of = {}, {}, {}, {}
+        factors_rest_of, factors_of, planes_of, codes_of, scales_of = {}, {}, {}, {}, {}
+        acc_of, h_of, relu_of, unit_of = {}, {}, {}, {}
         sum_squares_of, inv_norm_of, grouped_of = {}, {}, {}
 
-        def rows_of(group):
-            return slice(FIRST_TILE[group] * P, (FIRST_TILE[group] + GROUP_TILES[group]) * P)
-
-        def scalar_squares(group):
-            return SCALAR_SQUARES if GROUP_TILES[group] == TILES else 0
-
-        def vector_squares(group):
-            return GROUP_TILES[group] - scalar_squares(group)
-
-        def load_rows(group):
-            x = x_pool.tile([P, TILES, CHANNELS], BF16)
-            tiles = GROUP_TILES[group]
-            nc.sync.dma_start(
-                out=x[:, 0:tiles, :],
-                in_=pooled[rows_of(group), :].rearrange("(p r) k -> p r k", r=tiles),
-            )
-            x_of[group] = x
+        def tiles_on(table, group, engine):
+            roles = table.get(group, SQ_FULL if table is SQ else UN_FULL)
+            return [r for r in range(GROUP_TILES[group]) if roles[r] == engine]
 
         def row_statistics(group):
             mean_var = small.tile([P, TILES, 2], F32)
-            for r in range(GROUP_TILES[group]):
-                nc.vector.bn_stats(
-                    out=stats[:, FIRST_TILE[group] + r, 0, :], in_=x_of[group][:, r, :]
-                )
+            if group > 0:
+                own_statistics(group)
             for r in range(GROUP_TILES[group]):
                 nc.vector.bn_aggr(
                     out=mean_var[:, r, :],
@@ -217,15 +249,22 @@ def tile_textguidedcamfusion_pa_t_kernel(tc, pooled, proto, ln_g, ln_b, W, b, ou
             mean_var_of[group] = mean_var
 
         def inverse_std(group):
-            rstd = small.tile([P, TILES, QUADRANTS], F32)
             tiles = GROUP_TILES[group]
+            variance = mean_var_of[group][:, 0:tiles, 1]
+            rstd = small.tile([P, TILES], F32)
             nc.scalar.activation(
-                out=rstd[:, 0:tiles, 0:PARTS],
-                in_=mean_var_of[group][:, 0:tiles, 1].unsqueeze(2).to_broadcast([P, tiles, PARTS]),
-                func=ACT.Abs_reciprocal_sqrt,
-                bias=eps[:],
+                out=rstd[:, 0:tiles], in_=variance, func=ACT.Abs_reciprocal_sqrt, bias=eps[:]
             )
             rstd_of[group] = rstd
+            if group in PRODUCT_GROUPS:
+                factors_rest = small.tile([P, TILES, QUADRANTS], F32)
+                nc.scalar.activation(
+                    out=factors_rest[:, 0:tiles, 0:PARTS],
+                    in_=variance.unsqueeze(2).to_broadcast([P, tiles, PARTS]),
+                    func=ACT.Abs_reciprocal_sqrt,
+                    bias=eps[:],
+                )
+                factors_rest_of[group] = factors_rest
 
         def negate_mean(group):
             tiles = GROUP_TILES[group]
@@ -235,31 +274,42 @@ def tile_textguidedcamfusion_pa_t_kernel(tc, pooled, proto, ln_g, ln_b, W, b, ou
             )
             neg_mean_of[group] = neg_mean
 
-        def row_factors(group):
-            if group not in PRODUCT_GROUPS:
-                return
-            rest = rstd_of[group]
-            nc.gpsimd.tensor_tensor(
-                out=rest[:, :, SHIFT_QUADRANT],
-                in0=neg_mean_of[group][:],
-                in1=rest[:, :, 0],
-                op=ALU.mult,
-            )
-            factors = factor_tiles[group % 2]
-            for part in range(PARTS):
-                nc.gpsimd.tensor_copy(out=factors[:, :, :, part], in_=rest[:])
-                if part < PARTS - 1:
-                    smaller = small.tile([P, TILES, QUADRANTS], F32)
-                    nc.gpsimd.tensor_tensor(
-                        out=smaller[:], in0=rest[:], in1=factors[:, :, :, part], op=ALU.subtract
-                    )
-                    rest = smaller
+        def shift_factor(group):
+            if group in PRODUCT_GROUPS:
+                tiles = GROUP_TILES[group]
+                nc.vector.tensor_tensor(
+                    out=factors_rest_of[group][:, 0:tiles, SHIFT_QUADRANT],
+                    in0=neg_mean_of[group][:, 0:tiles],
+                    in1=rstd_of[group][:, 0:tiles],
+                    op=ALU.mult,
+                )
+
+        def round_factors(group, part):
+            if group in PRODUCT_GROUPS:
+                tiles = GROUP_TILES[group]
+                nc.vector.tensor_copy(
+                    out=factor_tiles[group % 2][:, 0:tiles, :, part],
+                    in_=factors_rest_of[group][:, 0:tiles, :],
+                )
+
+        def subtract_part(group, part):
+            if group in PRODUCT_GROUPS:
+                tiles = GROUP_TILES[group]
+                smaller = small.tile([P, TILES, QUADRANTS], F32)
+                nc.vector.tensor_tensor(
+                    out=smaller[:, 0:tiles, :],
+                    in0=factors_rest_of[group][:, 0:tiles, :],
+                    in1=factor_tiles[group % 2][:, 0:tiles, :, part],
+                    op=ALU.subtract,
+                )
+                factors_rest_of[group] = smaller
 
         def transpose_factors(group):
             if group not in PRODUCT_GROUPS:
                 return
             turned = psum_c.tile([P, TILES, P], BF16, tag="ctx")
-            for r in range(TILES):
+            tiles = GROUP_TILES[group]
+            for r in range(tiles):
                 nc.tensor.transpose(
                     turned[:, r, :],
                     factor_tiles[group % 2][:, r].rearrange("p q i -> p (q i)"),
@@ -267,8 +317,8 @@ def tile_textguidedcamfusion_pa_t_kernel(tc, pooled, proto, ln_g, ln_b, W, b, ou
                 )
             factors = z_pool.tile([P, TILES, P], BF16)
             nc.scalar.copy(
-                out=factors[:].rearrange("p r i -> p (r i)"),
-                in_=turned[:].rearrange("p r i -> p (r i)"),
+                out=factors[:, 0:tiles, :].rearrange("p r i -> p (r i)"),
+                in_=turned[:, 0:tiles, :].rearrange("p r i -> p (r i)"),
             )
             factors_of[group] = factors
 
@@ -286,16 +336,16 @@ def tile_textguidedcamfusion_pa_t_kernel(tc, pooled, proto, ln_g, ln_b, W, b, ou
                     out=u_of[group][:, r, half * CHANNELS : (half + 1) * CHANNELS],
                     in0=context[:] if half else x_of[group][:, r, :],
                     scalar1=neg_mean_of[group][:, r : r + 1],
-                    scalar2=rstd_of[group][:, r, 0:1],
+                    scalar2=rstd_of[group][:, r : r + 1],
                     op0=ALU.add,
                     op1=ALU.mult,
                 )
 
         def normalise_gpsimd(group):
-            normalise(group, nc.gpsimd, [piece for piece in pieces_of(group) if piece < GPSIMD_PIECES])
+            normalise(group, nc.gpsimd, pieces_of(group)[0:GPIECES.get(group, GPSIMD_PIECES)])
 
         def normalise_vector(group):
-            normalise(group, nc.vector, [piece for piece in pieces_of(group) if piece >= GPSIMD_PIECES])
+            normalise(group, nc.vector, pieces_of(group)[GPIECES.get(group, GPSIMD_PIECES):])
 
         def transpose_and_scale(group, blocks):
             if group not in planes_of:
@@ -319,7 +369,7 @@ def tile_textguidedcamfusion_pa_t_kernel(tc, pooled, proto, ln_g, ln_b, W, b, ou
 
         def grouped_tile(group):
             if group not in grouped_of:
-                z_grouped = grouped_pool.tile([P, PASSES, GROUP_ROWS, PACK], BF16, align_bytes=64)
+                z_grouped = grouped_pool.tile([P, PASSES, GROUP_TILES[group] * P, PACK], BF16, align_bytes=64)
                 grouped_of[group] = z_grouped
             return grouped_of[group]
 
@@ -327,7 +377,8 @@ def tile_textguidedcamfusion_pa_t_kernel(tc, pooled, proto, ln_g, ln_b, W, b, ou
             if group not in PRODUCT_GROUPS:
                 transpose_and_scale(group, [HALF_BLOCKS + part for part in parts])
                 return
-            z_grouped = grouped_tile(group)
+            if parts[0] >= GROUP_TILES[group]:
+                return
             for r in parts:
                 ctx = psum_c.tile([P, PACK, P], F32, tag="ctx")
                 for t in range(PACK):
@@ -339,7 +390,7 @@ def tile_textguidedcamfusion_pa_t_kernel(tc, pooled, proto, ln_g, ln_b, W, b, ou
                         stop=True,
                     )
                 nc.scalar.copy(
-                    out=z_grouped[:, 1, r * P : (r + 1) * P, :],
+                    out=grouped_tile(group)[:, 1, r * P : (r + 1) * P, :],
                     in_=ctx[:].rearrange("p t i -> p i t"),
                 )
 
@@ -347,26 +398,23 @@ def tile_textguidedcamfusion_pa_t_kernel(tc, pooled, proto, ln_g, ln_b, W, b, ou
             z_grouped = grouped_tile(group)
             rows = GROUP_TILES[group] * P
             for g in range(1 if group in PRODUCT_GROUPS else PASSES):
-                side_by_side(nc, z_grouped[:, g, 0:rows, :], planes_of[group][:, g, :, 0:rows])
+                side_by_side(
+                    nc.vector.tensor_copy,
+                    z_grouped[:, g, 0:rows, :],
+                    planes_of[group][:, g, :, 0:rows],
+                )
+
 
         def quantise(group):
             z_grouped = grouped_of[group]
-            z_codes = q_pool.tile([P, PASSES, GROUP_ROWS], U32, align_bytes=64)
-            z_scales = q_pool.tile([P, PASSES, GROUP_ROWS], U8, align_bytes=64)
             rows = GROUP_TILES[group] * P
-            if rows == GROUP_ROWS:
-                nc.vector.quantize_mx(
-                    out=z_codes[:].rearrange("p g c -> p (g c)").bitcast(FP8X4),
-                    scales=z_scales[:].rearrange("p g c -> p (g c)"),
-                    in_=z_grouped[:].rearrange("p g c t -> p (g c t)"),
-                )
-            else:
-                for g in range(PASSES):
-                    nc.vector.quantize_mx(
-                        out=z_codes[:, g, 0:rows].bitcast(FP8X4),
-                        scales=z_scales[:, g, 0:rows],
-                        in_=z_grouped[:, g, 0:rows, :].rearrange("p c t -> p (c t)"),
-                    )
+            z_codes = q_pool.tile([P, PASSES, rows], U32, align_bytes=64)
+            z_scales = q_pool.tile([P, PASSES, rows], U8, align_bytes=64)
+            nc.vector.quantize_mx(
+                out=z_codes[:].rearrange("p g c -> p (g c)").bitcast(FP8X4),
+                scales=z_scales[:].rearrange("p g c -> p (g c)"),
+                in_=z_grouped[:].rearrange("p g c t -> p (g c t)"),
+            )
             codes_of[group] = z_codes
             scales_of[group] = z_scales
 
@@ -387,18 +435,19 @@ def tile_textguidedcamfusion_pa_t_kernel(tc, pooled, proto, ln_g, ln_b, W, b, ou
                     )
                 acc_of[group, r] = acc
 
-        def add_bias(group):
-            h = h_pool.tile([P, TILES, D_OUT], F32)
-            for r in range(GROUP_TILES[group]):
+        def add_bias(group, r):
+            if group not in h_of:
+                h = h_pool.tile([P, TILES, D_OUT], F32)
+                h_of[group] = h
+                sum_squares = small.tile([P, TILES], F32)
+                sum_squares_of[group] = sum_squares
+            if r < GROUP_TILES[group]:
                 nc.vector.tensor_tensor(
-                    out=h[:, r, :], in0=acc_of[group, r][:], in1=bias_rows[:], op=ALU.add
+                    out=h_of[group][:, r, :], in0=acc_of[group, r][:], in1=bias_rows[:], op=ALU.add
                 )
-            h_of[group] = h
-            sum_squares = small.tile([P, TILES], F32)
-            sum_squares_of[group] = sum_squares
 
-        def squares_vector(group):
-            for r in range(vector_squares(group)):
+        def squares_vector(group, number):
+            for r in tiles_on(SQ, group, "V")[number : number + 1]:
                 squares = junk_pool.tile([P, D_OUT], BF16)
                 nc.vector.scalar_tensor_tensor(
                     out=squares[:],
@@ -411,52 +460,70 @@ def tile_textguidedcamfusion_pa_t_kernel(tc, pooled, proto, ln_g, ln_b, W, b, ou
                 )
 
         def squares_scalar(group):
-            tiles = range(vector_squares(group), GROUP_TILES[group])
-            if not tiles:
-                return
-            relu = junk_pool.tile([P, SCALAR_SQUARES, D_OUT], F32)
+            tiles = tiles_on(SQ, group, "S")
             for r in tiles:
-                nc.scalar.activation(
-                    out=relu[:, r - tiles.start, :], in_=h_of[group][:, r, :], func=ACT.Relu
-                )
+                relu = h_pool.tile([P, D_OUT], F32, name="relu_%d" % r)
+                relu_of[group, r] = relu
+                nc.scalar.activation(out=relu[:], in_=h_of[group][:, r, :], func=ACT.Relu)
             for r in tiles:
                 squares = junk_pool.tile([P, D_OUT], BF16, name="squares_scalar")
                 nc.scalar.activation(
                     out=squares[:],
-                    in_=relu[:, r - tiles.start, :],
+                    in_=relu_of[group, r][:],
                     func=ACT.Square,
                     accum_out=sum_squares_of[group][:, r : r + 1],
                 )
 
-        def floor_of_squares(group):
-            tiles = GROUP_TILES[group]
-            floored = small.tile([P, TILES], F32)
-            nc.vector.tensor_scalar_max(
-                out=floored[:, 0:tiles],
-                in0=sum_squares_of[group][:, 0:tiles],
-                scalar1=NORM_FLOOR**2,
-            )
-            sum_squares_of[group] = floored
-
         def inverse_norm(group):
             tiles = GROUP_TILES[group]
+            above = small.tile([P, TILES], F32)
+            nc.scalar.activation(
+                out=above[:, 0:tiles],
+                in_=sum_squares_of[group][:, 0:tiles],
+                func=ACT.Relu,
+                bias=floor[:, 0:1],
+            )
             inv_norm = small.tile([P, TILES], F32)
             nc.scalar.activation(
                 out=inv_norm[:, 0:tiles],
-                in_=sum_squares_of[group][:, 0:tiles],
+                in_=above[:, 0:tiles],
                 func=ACT.Abs_reciprocal_sqrt,
+                bias=floor[:, 1:2],
             )
             inv_norm_of[group] = inv_norm
             unit = o_pool.tile([P, TILES, D_OUT], F32)
             unit_of[group] = unit
 
-        def unit_rows(group, tiles):
-            for r in [r for r in tiles if r < GROUP_TILES[group]]:
-                nc.scalar.activation(
+        def unit_rows(group, half):
+            for r in tiles_on(UN, group, "S"):
+                if r // 2 == half:
+                    nc.scalar.activation(
+                        out=unit_of[group][:, r, :],
+                        in_=h_of[group][:, r, :],
+                        func=ACT.Relu,
+                        scale=inv_norm_of[group][:, r : r + 1],
+                    )
+
+        def unit_rows_vector(group):
+            for r in tiles_on(UN, group, "V"):
+                nc.vector.tensor_scalar(
                     out=unit_of[group][:, r, :],
-                    in_=h_of[group][:, r, :],
-                    func=ACT.Relu,
-                    scale=inv_norm_of[group][:, r : r + 1],
+                    in0=h_of[group][:, r, :],
+                    scalar1=0.0,
+                    scalar2=inv_norm_of[group][:, r : r + 1],
+                    op0=ALU.max,
+                    op1=ALU.mult,
+                )
+
+        def unit_rows_gpsimd(group):
+            for r in tiles_on(UN, group, "G"):
+                nc.gpsimd.tensor_scalar(
+                    out=unit_of[group][:, r, :],
+                    in0=relu_of[group, r][:],
+                    scalar1=inv_norm_of[group][:, r : r + 1],
+                    scalar2=0.0,
+                    op0=ALU.mult,
+                    op1=ALU.add,
                 )
 
         def store_unit_rows(group):
@@ -470,41 +537,68 @@ def tile_textguidedcamfusion_pa_t_kernel(tc, pooled, proto, ln_g, ln_b, W, b, ou
             if 0 <= group < GROUPS:
                 stage(group, *parts)
 
-        with tc.manual_schedule():
-            for step in range(-FIRST_STAGE_LEAD, GROUPS + LAST_STAGE_LAG + 1):
+        for step in range(-FIRST_STAGE_LEAD, GROUPS + LAST_STAGE_LAG + 1):
+            if step > -FIRST_STAGE_LEAD:
                 run(load_rows, step + FIRST_STAGE_LEAD)
-                if step == WEIGHTS_LOAD_STEP:
-                    load_weights()
-                if step == WEIGHTS_LOAD_STEP + 1:
-                    load_small_vectors()
-                run(floor_of_squares, step - 4)
-                run(negate_mean, step + 1)
-                run(normalise_gpsimd, step + 1)
-                run(row_factors, step + 1)
-                run(inverse_norm, step - 4)
-                run(add_bias, step - 3)
-                run(row_statistics, step + 2)
-                run(transpose_and_scale, step, (0, 1))
-                run(unit_rows, step - 4, (0, 1))
-                run(multiply, step - 2, (0,))
-                run(context_half, step, (0, 1))
-                run(multiply, step - 2, (1,))
-                run(squares_scalar, step - 3)
-                run(transpose_and_scale, step, (2, 3))
-                run(inverse_std, step + 2)
-                run(unit_rows, step - 4, (2, 3))
-                run(store_unit_rows, step - 4)
-                run(multiply, step - 2, (2,))
-                run(context_half, step, (2, 3))
-                run(multiply, step - 2, (3,))
-                if step == WEIGHTS_QUANTISE_STEP:
-                    quantise_weights()
-                if step == 0:
-                    clear_factors()
-                run(group_words, step - 1)
-                run(normalise_vector, step + 1)
-                run(squares_vector, step - 3)
-                if 1 <= step <= PARTS:
-                    features_part(step - 1)
-                run(quantise, step - 1)
-                run(transpose_factors, step + 1)
+            if step == WEIGHTS_LOAD_STEP:
+                load_weights()
+            if step == WEIGHTS_LOAD_STEP + 1:
+                load_small_vectors()
+            run(negate_mean, step + 1)
+            run(normalise_gpsimd, step + 1)
+            if A_FIRST:
+                for r in range(TILES):
+                    run(add_bias, step - LA, r)
+            run(row_statistics, step + 2)
+            run(transpose_and_scale, step, (0, 1))
+            for pos in range(4):
+                if MXPOS[pos] == 0:
+                    run(multiply, step - LM, (pos,))
+            run(inverse_norm, step - LC)
+            run(unit_rows, step - LC, 0)
+            run(unit_rows_gpsimd, step - LC)
+            run(context_half, step, (0, 1))
+            for pos in range(4):
+                if MXPOS[pos] == 1:
+                    run(multiply, step - LM, (pos,))
+            if Y_EARLY and A_FIRST:
+                run(squares_scalar, step - LA)
+            run(transpose_and_scale, step, (2, 3))
+            for pos in range(4):
+                if MXPOS[pos] == 2:
+                    run(multiply, step - LM, (pos,))
+            run(inverse_std, step + 2)
+            run(context_half, step, (2, 3))
+            run(unit_rows, step - LC, 1)
+            for pos in range(4):
+                if MXPOS[pos] == 3:
+                    run(multiply, step - LM, (pos,))
+            if not A_FIRST:
+                for r in range(TILES):
+                    run(add_bias, step - LA, r)
+            if not (Y_EARLY and A_FIRST):
+                run(squares_scalar, step - LA)
+            if 0 <= step < PASSES:
+                weight_words(step)
+            run(group_words, step - LQ)
+            run(normalise_vector, step + 1)
+            run(unit_rows_vector, step - LC)
+            run(store_unit_rows, step - LC)
+            run(shift_factor, step + 1)
+            run(squares_vector, step - LA, 0)
+            run(round_factors, step + 1, 0)
+            run(squares_vector, step - LA, 1)
+            run(squares_vector, step - LA, 2)
+            run(squares_vector, step - LA, 3)
+            run(subtract_part, step + 1, 0)
+            run(round_factors, step + 1, 1)
+            if 0 <= step < PARTS:
+                features_rest(step)
+                features_round(step)
+            run(quantise, step - LQ)
+            if step == 1:
+                for g in range(PASSES):
+                    quantise_weights(g)
+            run(subtract_part, step + 1, 1)
+            run(round_factors, step + 1, 2)
+            run(transpose_factors, step + 1)

@@ -37,11 +37,13 @@ LM = 2
 LA = 3
 LC = 4
 A_FIRST = True
-Y_EARLY = True
+Y_EARLY = False
 MXPOS = (0, 1, 2, 3)
-GPIECES = {0: 0}
+SCALAR_WORDS = (1,2)
+FACT = "G"
+GPIECES = {0:0,**{g:4 for g in range(4,17)}}
 SQ_FULL = "VVSS"
-UN_FULL = "VSSG"
+UN_FULL = "VVSS"
 SQ = {0: "SS", GROUPS - 1: "VV"}
 UN = {0: "SS", GROUPS - 1: "VS"}
 GPSIMD_PIECES = 5
@@ -277,7 +279,7 @@ def tile_textguidedcamfusion_pa_t_kernel(tc, pooled, proto, ln_g, ln_b, W, b, ou
         def shift_factor(group):
             if group in PRODUCT_GROUPS:
                 tiles = GROUP_TILES[group]
-                nc.vector.tensor_tensor(
+                (nc.gpsimd if FACT == "G" else nc.vector).tensor_tensor(
                     out=factors_rest_of[group][:, 0:tiles, SHIFT_QUADRANT],
                     in0=neg_mean_of[group][:, 0:tiles],
                     in1=rstd_of[group][:, 0:tiles],
@@ -287,7 +289,7 @@ def tile_textguidedcamfusion_pa_t_kernel(tc, pooled, proto, ln_g, ln_b, W, b, ou
         def round_factors(group, part):
             if group in PRODUCT_GROUPS:
                 tiles = GROUP_TILES[group]
-                nc.vector.tensor_copy(
+                (nc.gpsimd if FACT == "G" else nc.vector).tensor_copy(
                     out=factor_tiles[group % 2][:, 0:tiles, :, part],
                     in_=factors_rest_of[group][:, 0:tiles, :],
                 )
@@ -296,7 +298,7 @@ def tile_textguidedcamfusion_pa_t_kernel(tc, pooled, proto, ln_g, ln_b, W, b, ou
             if group in PRODUCT_GROUPS:
                 tiles = GROUP_TILES[group]
                 smaller = small.tile([P, TILES, QUADRANTS], F32)
-                nc.vector.tensor_tensor(
+                (nc.gpsimd if FACT == "G" else nc.vector).tensor_tensor(
                     out=smaller[:, 0:tiles, :],
                     in0=factors_rest_of[group][:, 0:tiles, :],
                     in1=factor_tiles[group % 2][:, 0:tiles, :, part],
@@ -397,11 +399,20 @@ def tile_textguidedcamfusion_pa_t_kernel(tc, pooled, proto, ln_g, ln_b, W, b, ou
         def group_words(group):
             z_grouped = grouped_tile(group)
             rows = GROUP_TILES[group] * P
-            for g in range(1 if group in PRODUCT_GROUPS else PASSES):
+            for g in range(1 if group in PRODUCT_GROUPS or group in SCALAR_WORDS else PASSES):
                 side_by_side(
                     nc.vector.tensor_copy,
                     z_grouped[:, g, 0:rows, :],
                     planes_of[group][:, g, :, 0:rows],
+                )
+
+        def context_words(group):
+            if group in SCALAR_WORDS:
+                rows = GROUP_TILES[group] * P
+                side_by_side(
+                    nc.scalar.copy,
+                    grouped_tile(group)[:, 1, 0:rows, :],
+                    planes_of[group][:, 1, :, 0:rows],
                 )
 
 
@@ -601,4 +612,5 @@ def tile_textguidedcamfusion_pa_t_kernel(tc, pooled, proto, ln_g, ln_b, W, b, ou
                     quantise_weights(g)
             run(subtract_part, step + 1, 1)
             run(round_factors, step + 1, 2)
+            run(context_words, step)
             run(transpose_factors, step + 1)

@@ -19,6 +19,7 @@ ROWS = 8192
 CHANNELS = 512
 FEATURES = 2 * CHANNELS
 D_OUT = 512
+D_BLOCKS = D_OUT // P
 PROTOS = 64
 PASSES = FEATURES // K_PASS
 BLOCKS = FEATURES // P
@@ -39,13 +40,15 @@ LC = 4
 A_FIRST = True
 Y_EARLY = False
 MXPOS = (0, 1, 2, 3)
-SCALAR_WORDS = (1,2)
+SCALAR_WORDS = ()
 FACT = "G"
-GPIECES = {0:0,**{g:4 for g in range(4,17)}}
-SQ_FULL = "VVSS"
-UN_FULL = "VVSS"
+GPIECES = {0:0,**{g:3 for g in range(4,17)}}
+SQ_FULL = "VVBB"
+UN_FULL = "VVVS"
 SQ = {0: "SS", GROUPS - 1: "VV"}
 UN = {0: "SS", GROUPS - 1: "VS"}
+Z_TILES = 2
+VRELU = ()
 GPSIMD_PIECES = 5
 SCALAR_SQUARES = 2
 STATS = 6
@@ -88,7 +91,8 @@ def tile_textguidedcamfusion_pa_t_kernel(tc, pooled, proto, ln_g, ln_b, W, b, ou
         o_pool = stack.enter_context(tc.tile_pool(name="o", bufs=2))
         psum_u = stack.enter_context(tc.psum_pool(name="psum_u", bufs=2))
         psum_c = stack.enter_context(tc.psum_pool(name="psum_c", bufs=2))
-        psum_acc = stack.enter_context(tc.psum_pool(name="psum_acc", bufs=4))
+        psum_acc = stack.enter_context(tc.psum_pool(name="psum_acc", bufs=2))
+        psum_back = stack.enter_context(tc.psum_pool(name="psum_back", bufs=2))
 
         stack.enter_context(tc.manual_schedule())
         x_of = {}
@@ -138,6 +142,11 @@ def tile_textguidedcamfusion_pa_t_kernel(tc, pooled, proto, ln_g, ln_b, W, b, ou
 
         own_statistics(0)
 
+        nc.sync.dma_start(
+            out=vector_rows[2 * BLOCKS : 2 * BLOCKS + D_BLOCKS, :],
+            in_=b.rearrange("(q p) -> q p", p=P),
+        )
+
         proto_sum = psum_acc.tile([P, CHANNELS], F32, tag="acc")
         nc.tensor.matmul(proto_sum[:], lhsT=ones[:], rhs=proto_rows[:], start=True, stop=True)
         context = const.tile([P, CHANNELS], F32)
@@ -154,8 +163,8 @@ def tile_textguidedcamfusion_pa_t_kernel(tc, pooled, proto, ln_g, ln_b, W, b, ou
         nc.scalar.copy(out=vector_rows_f32[:], in_=vector_rows[:])
         vector_cols = psum_u.tile([P, P], F32, tag="ut")
         nc.tensor.transpose(vector_cols[:], vector_rows_f32[:], identity[:])
-        per_partition = const.tile([P, 2 * BLOCKS], F32)
-        nc.scalar.copy(out=per_partition[:], in_=vector_cols[:, 0 : 2 * BLOCKS])
+        per_partition = const.tile([P, 2 * BLOCKS + D_BLOCKS], F32)
+        nc.scalar.copy(out=per_partition[:], in_=vector_cols[:, 0 : 2 * BLOCKS + D_BLOCKS])
 
         bias_rows = const.tile([P, D_OUT], BF16)
         gain_rows = const.tile([P, CHANNELS], BF16)
@@ -233,6 +242,7 @@ def tile_textguidedcamfusion_pa_t_kernel(tc, pooled, proto, ln_g, ln_b, W, b, ou
         mean_var_of, rstd_of, neg_mean_of, u_of = {}, {}, {}, {}
         factors_rest_of, factors_of, planes_of, codes_of, scales_of = {}, {}, {}, {}, {}
         acc_of, h_of, relu_of, unit_of = {}, {}, {}, {}
+        accw_of, relu_w_of, back_of = {}, {}, {}
         sum_squares_of, inv_norm_of, grouped_of = {}, {}, {}
 
         def tiles_on(table, group, engine):
@@ -431,7 +441,7 @@ def tile_textguidedcamfusion_pa_t_kernel(tc, pooled, proto, ln_g, ln_b, W, b, ou
 
         def multiply(group, tiles):
             for r in tiles:
-                if r >= GROUP_TILES[group]:
+                if r >= Z_TILES:
                     continue
                 acc = psum_acc.tile([P, D_OUT], F32, tag="acc")
                 for g in range(PASSES):
@@ -448,14 +458,98 @@ def tile_textguidedcamfusion_pa_t_kernel(tc, pooled, proto, ln_g, ln_b, W, b, ou
 
         def add_bias(group, r):
             if group not in h_of:
-                h = h_pool.tile([P, TILES, D_OUT], F32)
+                h = h_pool.tile([P, Z_TILES, D_OUT], F32)
                 h_of[group] = h
                 sum_squares = small.tile([P, TILES], F32)
                 sum_squares_of[group] = sum_squares
-            if r < GROUP_TILES[group]:
+            if r < Z_TILES:
                 nc.vector.tensor_tensor(
                     out=h_of[group][:, r, :], in0=acc_of[group, r][:], in1=bias_rows[:], op=ALU.add
                 )
+
+        def multiply_channels(group, pair):
+            if GROUP_TILES[group] < TILES:
+                return
+            if group not in relu_w_of:
+                relu_w = h_pool.tile([P, D_BLOCKS, Z_TILES * P], F32)
+                relu_w_of[group] = relu_w
+            rows = slice(Z_TILES * P, TILES * P)
+            accw = psum_c.tile([P, 2, Z_TILES * P], F32, tag="ctx")
+            for k in range(2):
+                d = 2 * pair + k
+                for g in range(PASSES):
+                    nc.tensor.matmul_mx(
+                        out=accw[:, k, :],
+                        lhsT=w_codes[:, g, d * P : (d + 1) * P].bitcast(FP8X4),
+                        lhsT_scale=w_scales[:, g, d * P : (d + 1) * P],
+                        rhs=codes_of[group][:, g, rows].bitcast(FP8X4),
+                        rhs_scale=scales_of[group][:, g, rows],
+                        start=(g == 0),
+                        stop=(g == PASSES - 1),
+                    )
+            accw_of[group, pair] = accw
+
+        def relu_channels(group, pair, engine):
+            if GROUP_TILES[group] < TILES:
+                return
+            for k in range(2):
+                d = 2 * pair + k
+                column = per_partition[:, 2 * BLOCKS + d : 2 * BLOCKS + d + 1]
+                if (d in VRELU) != (engine == "V"):
+                    continue
+                if engine == "V":
+                    nc.vector.tensor_scalar(
+                        out=relu_w_of[group][:, d, :],
+                        in0=accw_of[group, pair][:, k, :],
+                        scalar1=column,
+                        scalar2=0.0,
+                        op0=ALU.add,
+                        op1=ALU.max,
+                    )
+                else:
+                    nc.scalar.activation(
+                        out=relu_w_of[group][:, d, :],
+                        in_=accw_of[group, pair][:, k, :],
+                        func=ACT.Relu,
+                        bias=column,
+                    )
+
+        def rows_back(group):
+            if GROUP_TILES[group] < TILES:
+                return
+            for r in range(Z_TILES, TILES):
+                back = psum_back.tile([P, D_BLOCKS, P], F32, tag="back")
+                for d in range(D_BLOCKS):
+                    nc.tensor.transpose(
+                        back[:, d, :],
+                        relu_w_of[group][:, d, (r - Z_TILES) * P : (r - Z_TILES + 1) * P],
+                        identity[:],
+                    )
+                back_of[group, r] = back
+
+        def squares_back(group):
+            for r in tiles_on(SQ, group, "B"):
+                squares = junk_pool.tile([P, D_OUT], BF16, name="squares_back")
+                nc.scalar.activation(
+                    out=squares[:],
+                    in_=back_of[group, r][:].rearrange("p d i -> p (d i)"),
+                    func=ACT.Square,
+                    accum_out=sum_squares_of[group][:, r : r + 1],
+                )
+
+        def units_back(group, engine):
+            for r in tiles_on(UN, group, engine):
+                if r >= Z_TILES:
+                    back = back_of[group, r][:].rearrange("p d i -> p (d i)")
+                    scale = inv_norm_of[group][:, r : r + 1]
+                    if engine == "V":
+                        nc.vector.tensor_scalar_mul(
+                            out=unit_of[group][:, r, :], in0=back, scalar1=scale
+                        )
+                    else:
+                        nc.scalar.activation(
+                            out=unit_of[group][:, r, :], in_=back, func=ACT.Relu, scale=scale
+                        )
 
         def squares_vector(group, number):
             for r in tiles_on(SQ, group, "V")[number : number + 1]:
@@ -507,7 +601,7 @@ def tile_textguidedcamfusion_pa_t_kernel(tc, pooled, proto, ln_g, ln_b, W, b, ou
 
         def unit_rows(group, half):
             for r in tiles_on(UN, group, "S"):
-                if r // 2 == half:
+                if r < Z_TILES and r // 2 == half:
                     nc.scalar.activation(
                         out=unit_of[group][:, r, :],
                         in_=h_of[group][:, r, :],
@@ -516,7 +610,7 @@ def tile_textguidedcamfusion_pa_t_kernel(tc, pooled, proto, ln_g, ln_b, W, b, ou
                     )
 
         def unit_rows_vector(group):
-            for r in tiles_on(UN, group, "V"):
+            for r in [r for r in tiles_on(UN, group, "V") if r < Z_TILES]:
                 nc.vector.tensor_scalar(
                     out=unit_of[group][:, r, :],
                     in0=h_of[group][:, r, :],
@@ -557,60 +651,48 @@ def tile_textguidedcamfusion_pa_t_kernel(tc, pooled, proto, ln_g, ln_b, W, b, ou
                 load_small_vectors()
             run(negate_mean, step + 1)
             run(normalise_gpsimd, step + 1)
-            if A_FIRST:
-                for r in range(TILES):
-                    run(add_bias, step - LA, r)
+            run(shift_factor, step + 1)
+            for part in range(PARTS - 1):
+                run(round_factors, step + 1, part)
+                run(subtract_part, step + 1, part)
+            run(round_factors, step + 1, PARTS - 1)
+            for r in range(Z_TILES):
+                run(add_bias, step - 3, r)
             run(row_statistics, step + 2)
+            run(inverse_norm, step - 4)
             run(transpose_and_scale, step, (0, 1))
-            for pos in range(4):
-                if MXPOS[pos] == 0:
-                    run(multiply, step - LM, (pos,))
-            run(inverse_norm, step - LC)
-            run(unit_rows, step - LC, 0)
-            run(unit_rows_gpsimd, step - LC)
+            run(units_back, step - 4, "S")
+            run(units_back, step - 4, "V")
+            run(unit_rows, step - 4, 0)
             run(context_half, step, (0, 1))
-            for pos in range(4):
-                if MXPOS[pos] == 1:
-                    run(multiply, step - LM, (pos,))
-            if Y_EARLY and A_FIRST:
-                run(squares_scalar, step - LA)
-            run(transpose_and_scale, step, (2, 3))
-            for pos in range(4):
-                if MXPOS[pos] == 2:
-                    run(multiply, step - LM, (pos,))
+            run(multiply, step - 2, (0,))
+            run(rows_back, step - 3)
+            run(multiply, step - 2, (1,))
+            run(multiply_channels, step - 2, 0)
+            run(relu_channels, step - 2, 0, "V")
             run(inverse_std, step + 2)
+            run(squares_back, step - 3)
+            run(relu_channels, step - 2, 0, "S")
+            run(transpose_and_scale, step, (2, 3))
+            run(multiply_channels, step - 2, 1)
+            run(relu_channels, step - 2, 1, "V")
+            run(relu_channels, step - 2, 1, "S")
             run(context_half, step, (2, 3))
-            run(unit_rows, step - LC, 1)
-            for pos in range(4):
-                if MXPOS[pos] == 3:
-                    run(multiply, step - LM, (pos,))
-            if not A_FIRST:
-                for r in range(TILES):
-                    run(add_bias, step - LA, r)
-            if not (Y_EARLY and A_FIRST):
-                run(squares_scalar, step - LA)
+            run(squares_scalar, step - 3)
             if 0 <= step < PASSES:
                 weight_words(step)
-            run(group_words, step - LQ)
+            run(group_words, step - 1)
             run(normalise_vector, step + 1)
-            run(unit_rows_vector, step - LC)
-            run(store_unit_rows, step - LC)
-            run(shift_factor, step + 1)
-            run(squares_vector, step - LA, 0)
-            run(round_factors, step + 1, 0)
-            run(squares_vector, step - LA, 1)
-            run(squares_vector, step - LA, 2)
-            run(squares_vector, step - LA, 3)
-            run(subtract_part, step + 1, 0)
-            run(round_factors, step + 1, 1)
+            run(unit_rows_vector, step - 4)
+            run(store_unit_rows, step - 4)
+            run(squares_vector, step - 3, 0)
+            run(squares_vector, step - 3, 1)
             if 0 <= step < PARTS:
                 features_rest(step)
                 features_round(step)
-            run(quantise, step - LQ)
+            run(quantise, step - 1)
             if step == 1:
                 for g in range(PASSES):
                     quantise_weights(g)
-            run(subtract_part, step + 1, 1)
-            run(round_factors, step + 1, 2)
             run(context_words, step)
             run(transpose_factors, step + 1)

@@ -33,20 +33,12 @@ ROW_TILES = ROWS // P
 FIRST_FULL = 3
 assert sum(GROUP_TILES) == ROW_TILES
 PRODUCT_GROUPS = range(4, 17)
-LQ = 1
-LM = 2
-LA = 3
-LC = 4
-A_FIRST = True
-Y_EARLY = False
-MXPOS = (0, 1, 2, 3)
 SCALAR_WORDS = ()
-FACT = "G"
 GPIECES = {0:0,**{g:3 for g in range(4,17)}}
 SQ_FULL = "VVBB"
 UN_FULL = "VVVS"
 SQ = {0: "SS", GROUPS - 1: "VV"}
-UN = {0: "SS", GROUPS - 1: "VS"}
+UN = {0:"SS",GROUPS-1:"VS",15:"VVSS"}
 Z_TILES = 2
 VRELU = ()
 GPSIMD_PIECES = 5
@@ -286,35 +278,29 @@ def tile_textguidedcamfusion_pa_t_kernel(tc, pooled, proto, ln_g, ln_b, W, b, ou
             )
             neg_mean_of[group] = neg_mean
 
-        def shift_factor(group):
-            if group in PRODUCT_GROUPS:
-                tiles = GROUP_TILES[group]
-                (nc.gpsimd if FACT == "G" else nc.vector).tensor_tensor(
-                    out=factors_rest_of[group][:, 0:tiles, SHIFT_QUADRANT],
-                    in0=neg_mean_of[group][:, 0:tiles],
-                    in1=rstd_of[group][:, 0:tiles],
-                    op=ALU.mult,
-                )
-
-        def round_factors(group, part):
-            if group in PRODUCT_GROUPS:
-                tiles = GROUP_TILES[group]
-                (nc.gpsimd if FACT == "G" else nc.vector).tensor_copy(
-                    out=factor_tiles[group % 2][:, 0:tiles, :, part],
-                    in_=factors_rest_of[group][:, 0:tiles, :],
-                )
-
-        def subtract_part(group, part):
-            if group in PRODUCT_GROUPS:
-                tiles = GROUP_TILES[group]
-                smaller = small.tile([P, TILES, QUADRANTS], F32)
-                (nc.gpsimd if FACT == "G" else nc.vector).tensor_tensor(
-                    out=smaller[:, 0:tiles, :],
-                    in0=factors_rest_of[group][:, 0:tiles, :],
-                    in1=factor_tiles[group % 2][:, 0:tiles, :, part],
-                    op=ALU.subtract,
-                )
-                factors_rest_of[group] = smaller
+        def row_factors(group):
+            if group not in PRODUCT_GROUPS:
+                return
+            tiles = GROUP_TILES[group]
+            rest = factors_rest_of[group]
+            nc.gpsimd.tensor_tensor(
+                out=rest[:, 0:tiles, SHIFT_QUADRANT],
+                in0=neg_mean_of[group][:, 0:tiles],
+                in1=rstd_of[group][:, 0:tiles],
+                op=ALU.mult,
+            )
+            factors = factor_tiles[group % 2]
+            for part in range(PARTS):
+                nc.gpsimd.tensor_copy(out=factors[:, 0:tiles, :, part], in_=rest[:, 0:tiles, :])
+                if part < PARTS - 1:
+                    smaller = small.tile([P, TILES, QUADRANTS], F32)
+                    nc.gpsimd.tensor_tensor(
+                        out=smaller[:, 0:tiles, :],
+                        in0=rest[:, 0:tiles, :],
+                        in1=factors[:, 0:tiles, :, part],
+                        op=ALU.subtract,
+                    )
+                    rest = smaller
 
         def transpose_factors(group):
             if group not in PRODUCT_GROUPS:
@@ -651,11 +637,7 @@ def tile_textguidedcamfusion_pa_t_kernel(tc, pooled, proto, ln_g, ln_b, W, b, ou
                 load_small_vectors()
             run(negate_mean, step + 1)
             run(normalise_gpsimd, step + 1)
-            run(shift_factor, step + 1)
-            for part in range(PARTS - 1):
-                run(round_factors, step + 1, part)
-                run(subtract_part, step + 1, part)
-            run(round_factors, step + 1, PARTS - 1)
+            run(row_factors, step + 1)
             for r in range(Z_TILES):
                 run(add_bias, step - 3, r)
             run(row_statistics, step + 2)
@@ -665,19 +647,17 @@ def tile_textguidedcamfusion_pa_t_kernel(tc, pooled, proto, ln_g, ln_b, W, b, ou
             run(units_back, step - 4, "V")
             run(unit_rows, step - 4, 0)
             run(context_half, step, (0, 1))
+            run(transpose_and_scale, step, (2, 3))
             run(multiply, step - 2, (0,))
-            run(rows_back, step - 3)
+            run(context_half, step, (2, 3))
             run(multiply, step - 2, (1,))
+            run(rows_back, step - 3)
             run(multiply_channels, step - 2, 0)
-            run(relu_channels, step - 2, 0, "V")
-            run(inverse_std, step + 2)
             run(squares_back, step - 3)
             run(relu_channels, step - 2, 0, "S")
-            run(transpose_and_scale, step, (2, 3))
             run(multiply_channels, step - 2, 1)
-            run(relu_channels, step - 2, 1, "V")
+            run(inverse_std, step + 2)
             run(relu_channels, step - 2, 1, "S")
-            run(context_half, step, (2, 3))
             run(squares_scalar, step - 3)
             if 0 <= step < PASSES:
                 weight_words(step)

@@ -81,8 +81,7 @@ def tile_textguidedcamfusion_pa_t_kernel(tc, pooled, proto, ln_g, ln_b, W, b, ou
         h_pool = stack.enter_context(tc.tile_pool(name="h", bufs=3))
         junk_pool = stack.enter_context(tc.tile_pool(name="junk", bufs=2))
         o_pool = stack.enter_context(tc.tile_pool(name="o", bufs=2))
-        psum_u = stack.enter_context(tc.psum_pool(name="psum_u", bufs=2))
-        psum_c = stack.enter_context(tc.psum_pool(name="psum_c", bufs=2))
+        psum_s = stack.enter_context(tc.psum_pool(name="psum_s", bufs=4))
         psum_acc = stack.enter_context(tc.psum_pool(name="psum_acc", bufs=2))
         psum_back = stack.enter_context(tc.psum_pool(name="psum_back", bufs=2))
 
@@ -153,7 +152,7 @@ def tile_textguidedcamfusion_pa_t_kernel(tc, pooled, proto, ln_g, ln_b, W, b, ou
 
         vector_rows_f32 = const.tile([P, P], F32)
         nc.scalar.copy(out=vector_rows_f32[:], in_=vector_rows[:])
-        vector_cols = psum_u.tile([P, P], F32, tag="ut")
+        vector_cols = psum_s.tile([P, P], F32, tag="stream")
         nc.tensor.transpose(vector_cols[:], vector_rows_f32[:], identity[:])
         per_partition = const.tile([P, 2 * BLOCKS + D_BLOCKS], F32)
         nc.scalar.copy(out=per_partition[:], in_=vector_cols[:, 0 : 2 * BLOCKS + D_BLOCKS])
@@ -305,7 +304,7 @@ def tile_textguidedcamfusion_pa_t_kernel(tc, pooled, proto, ln_g, ln_b, W, b, ou
         def transpose_factors(group):
             if group not in PRODUCT_GROUPS:
                 return
-            turned = psum_c.tile([P, TILES, P], BF16, tag="ctx")
+            turned = psum_s.tile([P, TILES, P], BF16, tag="stream")
             tiles = GROUP_TILES[group]
             for r in range(tiles):
                 nc.tensor.transpose(
@@ -351,8 +350,7 @@ def tile_textguidedcamfusion_pa_t_kernel(tc, pooled, proto, ln_g, ln_b, W, b, ou
                 planes_of[group] = z_planes
             tiles = GROUP_TILES[group]
             for block in blocks:
-                pool, tag = (psum_c, "ctx") if block >= HALF_BLOCKS else (psum_u, "ut")
-                ut = pool.tile([P, TILES, P], F32, tag=tag, name="ut")
+                ut = psum_s.tile([P, TILES, P], F32, tag="stream", name="ut")
                 for r in range(tiles):
                     nc.tensor.transpose(
                         ut[:, r, :], u_of[group][:, r, block * P : (block + 1) * P], identity[:]
@@ -378,7 +376,7 @@ def tile_textguidedcamfusion_pa_t_kernel(tc, pooled, proto, ln_g, ln_b, W, b, ou
             if parts[0] >= GROUP_TILES[group]:
                 return
             for r in parts:
-                ctx = psum_c.tile([P, PACK, P], F32, tag="ctx")
+                ctx = psum_s.tile([P, PACK, P], F32, tag="stream")
                 for t in range(PACK):
                     nc.tensor.matmul(
                         ctx[:, t, :],
@@ -460,7 +458,7 @@ def tile_textguidedcamfusion_pa_t_kernel(tc, pooled, proto, ln_g, ln_b, W, b, ou
                 relu_w = h_pool.tile([P, D_BLOCKS, Z_TILES * P], F32)
                 relu_w_of[group] = relu_w
             rows = slice(Z_TILES * P, TILES * P)
-            accw = psum_c.tile([P, 2, Z_TILES * P], F32, tag="ctx")
+            accw = psum_s.tile([P, 2, Z_TILES * P], F32, tag="stream")
             for k in range(2):
                 d = 2 * pair + k
                 for g in range(PASSES):
@@ -647,8 +645,8 @@ def tile_textguidedcamfusion_pa_t_kernel(tc, pooled, proto, ln_g, ln_b, W, b, ou
             run(units_back, step - 4, "V")
             run(unit_rows, step - 4, 0)
             run(context_half, step, (0, 1))
-            run(transpose_and_scale, step, (2, 3))
             run(multiply, step - 2, (0,))
+            run(transpose_and_scale, step, (2, 3))
             run(context_half, step, (2, 3))
             run(multiply, step - 2, (1,))
             run(rows_back, step - 3)

from contextlib import ExitStack

import concourse.mybir as mybir
from concourse.masks import make_identity

F32 = mybir.dt.float32
BF16 = mybir.dt.bfloat16
U32 = mybir.dt.uint32
U8 = mybir.dt.uint8
FP8X4 = mybir.dt.float8_e4m3fn_x4
ALU = mybir.AluOpType
ACT = mybir.ActivationFunctionType

P = 128
PACK = 4
K_PASS = P * PACK

ROWS = 8192
CHANNELS = 512
FEATURES = 2 * CHANNELS
D_OUT = 512
D_BLOCKS = D_OUT // P
PROTOS = 64
PASSES = FEATURES // K_PASS
BLOCKS = FEATURES // P
HALF_BLOCKS = CHANNELS // P
TILES = 4
GROUP_ROWS = TILES * P
GROUP_TILES = (2,) + (TILES,) * 15 + (2,)
GROUPS = len(GROUP_TILES)
FIRST_TILE = [sum(GROUP_TILES[:group]) for group in range(GROUPS)]
ROW_TILES = ROWS // P
FIRST_FULL = 3
assert sum(GROUP_TILES) == ROW_TILES
PRODUCT_GROUPS = range(4, 17)
SCALAR_WORDS = ()
GPIECES = {0:0,**{g:3 for g in range(4,17)}}
SQ_FULL = "VVBB"
UN_FULL = "VVVS"
SQ = {0: "SS", GROUPS - 1: "VV"}
UN = {0:"SS",GROUPS-1:"VS",15:"VVSS"}
Z_TILES = 2
VRELU = ()
GPSIMD_PIECES = 5
SCALAR_SQUARES = 2
STATS = 6
LN_EPS = 1e-5
NORM_FLOOR = 1e-12
FIRST_STAGE_LEAD = 4
LAST_STAGE_LAG = 4

QUADRANT = 32
QUADRANTS = P // QUADRANT
PARTS = 3
SHIFT_QUADRANT = 3
ONE_ROW = SHIFT_QUADRANT * QUADRANT + QUADRANT // 2

WEIGHTS_LOAD_STEP = -2
WEIGHTS_QUANTISE_STEP = 0

FLOPS = 2 * ROWS * FEATURES * D_OUT


def side_by_side(copy, grouped, planes):
    copy(
        out=grouped.rearrange("p (c i) t -> p c t i", i=4),
        in_=planes.rearrange("p t (c i) -> p c t i", i=4),
    )


def tile_textguidedcamfusion_pa_t_kernel(tc, pooled, proto, ln_g, ln_b, W, b, out):
    nc = tc.nc
    with ExitStack() as stack:
        const = stack.enter_context(tc.tile_pool(name="const", bufs=1))
        x_pool = stack.enter_context(tc.tile_pool(name="x", bufs=5))
        small = stack.enter_context(tc.tile_pool(name="small", bufs=4))
        u_pool = stack.enter_context(tc.tile_pool(name="u", bufs=2))
        z_pool = stack.enter_context(tc.tile_pool(name="z", bufs=2))
        grouped_pool = stack.enter_context(tc.tile_pool(name="grouped", bufs=3))
        q_pool = stack.enter_context(tc.tile_pool(name="q", bufs=3))
        h_pool = stack.enter_context(tc.tile_pool(name="h", bufs=3))
        junk_pool = stack.enter_context(tc.tile_pool(name="junk", bufs=2))
        o_pool = stack.enter_context(tc.tile_pool(name="o", bufs=2))
        psum_s = stack.enter_context(tc.psum_pool(name="psum_s", bufs=4))
        psum_acc = stack.enter_context(tc.psum_pool(name="psum_acc", bufs=2))
        psum_back = stack.enter_context(tc.psum_pool(name="psum_back", bufs=2))

        stack.enter_context(tc.manual_schedule())
        x_of = {}

        def rows_of(group):
            return slice(FIRST_TILE[group] * P, (FIRST_TILE[group] + GROUP_TILES[group]) * P)

        def load_rows(group):
            x = x_pool.tile([P, TILES, CHANNELS], BF16)
            tiles = GROUP_TILES[group]
            nc.sync.dma_start(
                out=x[:, 0:tiles, :],
                in_=pooled[rows_of(group), :].rearrange("(p r) k -> p r k", r=tiles),
            )
            x_of[group] = x

        ones = const.tile([P, P], BF16)
        nc.vector.memset(ones[:], 1.0)
        proto_rows = const.tile([P, CHANNELS], BF16)
        nc.vector.memset(proto_rows[PROTOS:P, :], 0.0)
        vector_rows = const.tile([P, P], BF16)
        nc.vector.memset(vector_rows[:], 0.0)
        eps = const.tile([P, 1], F32)
        nc.vector.memset(eps[:], LN_EPS)
        floor = const.tile([P, 2], F32)
        nc.vector.memset(floor[:, 0:1], -(NORM_FLOOR**2))
        nc.vector.memset(floor[:, 1:2], NORM_FLOOR**2)
        identity = const.tile([P, P], F32)
        make_identity(nc, identity[:])
        identity_bf16 = const.tile([P, P], BF16)
        nc.gpsimd.tensor_copy(out=identity_bf16[:], in_=identity[:])

        load_rows(0)
        nc.sync.dma_start(out=proto_rows[0:PROTOS, :], in_=proto)
        nc.sync.dma_start(out=vector_rows[0:BLOCKS, :], in_=ln_g.rearrange("(q p) -> q p", p=P))
        nc.sync.dma_start(
            out=vector_rows[BLOCKS : 2 * BLOCKS, :], in_=ln_b.rearrange("(q p) -> q p", p=P)
        )

        stats = const.tile([P, ROW_TILES, 2, STATS], F32)

        def own_statistics(group):
            for r in range(GROUP_TILES[group]):
                nc.vector.bn_stats(
                    out=stats[:, FIRST_TILE[group] + r, 0, :], in_=x_of[group][:, r, :]
                )

        own_statistics(0)

        nc.sync.dma_start(
            out=vector_rows[2 * BLOCKS : 2 * BLOCKS + D_BLOCKS, :],
            in_=b.rearrange("(q p) -> q p", p=P),
        )

        proto_sum = psum_acc.tile([P, CHANNELS], F32, tag="acc")
        nc.tensor.matmul(proto_sum[:], lhsT=ones[:], rhs=proto_rows[:], start=True, stop=True)
        context = const.tile([P, CHANNELS], F32)
        nc.vector.tensor_scalar_mul(out=context[:], in0=proto_sum[:], scalar1=1.0 / PROTOS)

        context_stats = const.tile([P, STATS], F32)
        nc.vector.bn_stats(out=context_stats[:], in_=context[:])
        nc.vector.tensor_copy(
            out=stats[:, :, 1, :],
            in_=context_stats[:].unsqueeze(1).to_broadcast([P, ROW_TILES, STATS]),
        )

        vector_rows_f32 = const.tile([P, P], F32)
        nc.scalar.copy(out=vector_rows_f32[:], in_=vector_rows[:])
        vector_cols = psum_s.tile([P, P], F32, tag="stream")
        nc.tensor.transpose(vector_cols[:], vector_rows_f32[:], identity[:])
        per_partition = const.tile([P, 2 * BLOCKS + D_BLOCKS], F32)
        nc.scalar.copy(out=per_partition[:], in_=vector_cols[:, 0 : 2 * BLOCKS + D_BLOCKS])

        bias_rows = const.tile([P, D_OUT], BF16)
        gain_rows = const.tile([P, CHANNELS], BF16)
        features_side = const.tile([P, CHANNELS], BF16)
        factor_tiles = [
            const.tile([P, TILES, QUADRANTS, QUADRANT], BF16, name="factors_even"),
            const.tile([P, TILES, QUADRANTS, QUADRANT], BF16, name="factors_odd"),
        ]

        def load_small_vectors():
            nc.sync.dma_start(out=bias_rows[:], in_=b.partition_broadcast(P))
            nc.sync.dma_start(
                out=gain_rows[:], in_=ln_g[CHANNELS:FEATURES].partition_broadcast(P)
            )
            nc.sync.dma_start(
                out=features_side[SHIFT_QUADRANT * QUADRANT : ONE_ROW, :],
                in_=ln_g[CHANNELS:FEATURES].partition_broadcast(QUADRANT // 2),
            )
            nc.sync.dma_start(
                out=features_side[ONE_ROW:P, :],
                in_=ln_b[CHANNELS:FEATURES].partition_broadcast(QUADRANT // 2),
            )

        def clear_factors():
            for factors in factor_tiles:
                nc.gpsimd.memset(factors[:], 0.0)
                nc.gpsimd.memset(factors[:, :, SHIFT_QUADRANT, QUADRANT // 2], 1.0)

        rest_of = {}

        def features_rest(part):
            rest = const.tile([P, CHANNELS], F32, name="rest_%d" % part)
            if part == 0:
                nc.vector.tensor_tensor(
                    out=rest[:], in0=context[:], in1=gain_rows[:], op=ALU.mult
                )
            else:
                before, rounded = rest_of[part - 1]
                nc.vector.tensor_tensor(
                    out=rest[:], in0=before[:], in1=rounded[:], op=ALU.subtract
                )
            rest_of[part] = rest

        def features_round(part):
            rest = rest_of[part]
            rows = slice(part * QUADRANT, (part + 1) * QUADRANT)
            nc.scalar.copy(out=features_side[rows, :], in_=rest[rows, :])
            if part < PARTS - 1:
                rounded = const.tile([P, CHANNELS], BF16, name="rounded_%d" % part)
                nc.scalar.copy(out=rounded[:], in_=rest[:])
                rest_of[part] = (rest, rounded)

        clear_factors()

        w_planes = const.tile([P, PASSES, PACK, D_OUT], BF16)
        w_grouped = const.tile([P, PASSES, D_OUT, PACK], BF16, align_bytes=64)
        w_codes = const.tile([P, PASSES, D_OUT], U32, align_bytes=64)
        w_scales = const.tile([P, PASSES, D_OUT], U8, align_bytes=64)

        def load_weights():
            nc.sync.dma_start(
                out=w_planes[:], in_=W.rearrange("(g t p) d -> p g t d", t=PACK, p=P)
            )

        def weight_words(g):
            side_by_side(nc.scalar.copy, w_grouped[:, g], w_planes[:, g])

        def quantise_weights(g):
            nc.vector.quantize_mx(
                out=w_codes[:, g, :].bitcast(FP8X4),
                scales=w_scales[:, g, :],
                in_=w_grouped[:, g].rearrange("p d t -> p (d t)"),
            )

        mean_var_of, rstd_of, neg_mean_of, u_of = {}, {}, {}, {}
        factors_rest_of, factors_of, planes_of, codes_of, scales_of = {}, {}, {}, {}, {}
        acc_of, h_of, relu_of, unit_of = {}, {}, {}, {}
        accw_of, relu_w_of, back_of = {}, {}, {}
        sum_squares_of, inv_norm_of, grouped_of = {}, {}, {}

        def tiles_on(table, group, engine):
            roles = table.get(group, SQ_FULL if table is SQ else UN_FULL)
            return [r for r in range(GROUP_TILES[group]) if roles[r] == engine]

        def row_statistics(group):
            mean_var = small.tile([P, TILES, 2], F32)
            if group > 0:
                own_statistics(group)
            for r in range(GROUP_TILES[group]):
                nc.vector.bn_aggr(
                    out=mean_var[:, r, :],
                    in_=stats[:, FIRST_TILE[group] + r, :, :].rearrange("p a s -> p (a s)"),
                )
            mean_var_of[group] = mean_var

        def inverse_std(group):
            tiles = GROUP_TILES[group]
            variance = mean_var_of[group][:, 0:tiles, 1]
            rstd = small.tile([P, TILES], F32)
            nc.scalar.activation(
                out=rstd[:, 0:tiles], in_=variance, func=ACT.Abs_reciprocal_sqrt, bias=eps[:]
            )
            rstd_of[group] = rstd
            if group in PRODUCT_GROUPS:
                factors_rest = small.tile([P, TILES, QUADRANTS], F32)
                nc.scalar.activation(
                    out=factors_rest[:, 0:tiles, 0:PARTS],
                    in_=variance.unsqueeze(2).to_broadcast([P, tiles, PARTS]),
                    func=ACT.Abs_reciprocal_sqrt,
                    bias=eps[:],
                )
                factors_rest_of[group] = factors_rest

        def negate_mean(group):
            tiles = GROUP_TILES[group]
            neg_mean = small.tile([P, TILES], F32)
            nc.vector.tensor_scalar_mul(
                out=neg_mean[:, 0:tiles], in0=mean_var_of[group][:, 0:tiles, 0], scalar1=-1.0
            )
            neg_mean_of[group] = neg_mean

        def row_factors(group):
            if group not in PRODUCT_GROUPS:
                return
            tiles = GROUP_TILES[group]
            rest = factors_rest_of[group]
            nc.gpsimd.tensor_tensor(
                out=rest[:, 0:tiles, SHIFT_QUADRANT],
                in0=neg_mean_of[group][:, 0:tiles],
                in1=rstd_of[group][:, 0:tiles],
                op=ALU.mult,
            )
            factors = factor_tiles[group % 2]
            for part in range(PARTS):
                nc.gpsimd.tensor_copy(out=factors[:, 0:tiles, :, part], in_=rest[:, 0:tiles, :])
                if part < PARTS - 1:
                    smaller = small.tile([P, TILES, QUADRANTS], F32)
                    nc.gpsimd.tensor_tensor(
                        out=smaller[:, 0:tiles, :],
                        in0=rest[:, 0:tiles, :],
                        in1=factors[:, 0:tiles, :, part],
                        op=ALU.subtract,
                    )
                    rest = smaller

        def transpose_factors(group):
            if group not in PRODUCT_GROUPS:
                return
            turned = psum_s.tile([P, TILES, P], BF16, tag="stream")
            tiles = GROUP_TILES[group]
            for r in range(tiles):
                nc.tensor.transpose(
                    turned[:, r, :],
                    factor_tiles[group % 2][:, r].rearrange("p q i -> p (q i)"),
                    identity_bf16[:],
                )
            factors = z_pool.tile([P, TILES, P], BF16)
            nc.scalar.copy(
                out=factors[:, 0:tiles, :].rearrange("p r i -> p (r i)"),
                in_=turned[:, 0:tiles, :].rearrange("p r i -> p (r i)"),
            )
            factors_of[group] = factors

        def pieces_of(group):
            step = 2 if group in PRODUCT_GROUPS else 1
            return list(range(0, 2 * GROUP_TILES[group], step))

        def normalise(group, engine, pieces):
            if group not in u_of:
                u = u_pool.tile([P, TILES, FEATURES], F32)
                u_of[group] = u
            for piece in pieces:
                r, half = divmod(piece, 2)
                engine.tensor_scalar(
                    out=u_of[group][:, r, half * CHANNELS : (half + 1) * CHANNELS],
                    in0=context[:] if half else x_of[group][:, r, :],
                    scalar1=neg_mean_of[group][:, r : r + 1],
                    scalar2=rstd_of[group][:, r : r + 1],
                    op0=ALU.add,
                    op1=ALU.mult,
                )

        def normalise_gpsimd(group):
            normalise(group, nc.gpsimd, pieces_of(group)[0:GPIECES.get(group, GPSIMD_PIECES)])

        def normalise_vector(group):
            normalise(group, nc.vector, pieces_of(group)[GPIECES.get(group, GPSIMD_PIECES):])

        def transpose_and_scale(group, blocks):
            if group not in planes_of:
                z_planes = z_pool.tile([P, PASSES, PACK, GROUP_ROWS], BF16)
                planes_of[group] = z_planes
            tiles = GROUP_TILES[group]
            for block in blocks:
                ut = psum_s.tile([P, TILES, P], F32, tag="stream", name="ut")
                for r in range(tiles):
                    nc.tensor.transpose(
                        ut[:, r, :], u_of[group][:, r, block * P : (block + 1) * P], identity[:]
                    )
                nc.scalar.activation(
                    out=planes_of[group][:, block // PACK, block % PACK, 0 : tiles * P],
                    in_=ut[:, 0:tiles, :].rearrange("p r i -> p (r i)"),
                    func=ACT.Identity,
                    scale=per_partition[:, block : block + 1],
                    bias=per_partition[:, BLOCKS + block : BLOCKS + block + 1],
                )

        def grouped_tile(group):
            if group not in grouped_of:
                z_grouped = grouped_pool.tile([P, PASSES, GROUP_TILES[group] * P, PACK], BF16, align_bytes=64)
                grouped_of[group] = z_grouped
            return grouped_of[group]

        def context_half(group, parts):
            if group not in PRODUCT_GROUPS:
                transpose_and_scale(group, [HALF_BLOCKS + part for part in parts])
                return
            if parts[0] >= GROUP_TILES[group]:
                return
            for r in parts:
                ctx = psum_s.tile([P, PACK, P], F32, tag="stream")
                for t in range(PACK):
                    nc.tensor.matmul(
                        ctx[:, t, :],
                        lhsT=features_side[:, t * P : (t + 1) * P],
                        rhs=factors_of[group][:, r, :],
                        start=True,
                        stop=True,
                    )
                nc.scalar.copy(
                    out=grouped_tile(group)[:, 1, r * P : (r + 1) * P, :],
                    in_=ctx[:].rearrange("p t i -> p i t"),
                )

        def group_words(group):
            z_grouped = grouped_tile(group)
            rows = GROUP_TILES[group] * P
            for g in range(1 if group in PRODUCT_GROUPS or group in SCALAR_WORDS else PASSES):
                side_by_side(
                    nc.vector.tensor_copy,
                    z_grouped[:, g, 0:rows, :],
                    planes_of[group][:, g, :, 0:rows],
                )

        def context_words(group):
            if group in SCALAR_WORDS:
                rows = GROUP_TILES[group] * P
                side_by_side(
                    nc.scalar.copy,
                    grouped_tile(group)[:, 1, 0:rows, :],
                    planes_of[group][:, 1, :, 0:rows],
                )


        def quantise(group):
            z_grouped = grouped_of[group]
            rows = GROUP_TILES[group] * P
            z_codes = q_pool.tile([P, PASSES, rows], U32, align_bytes=64)
            z_scales = q_pool.tile([P, PASSES, rows], U8, align_bytes=64)
            nc.vector.quantize_mx(
                out=z_codes[:].rearrange("p g c -> p (g c)").bitcast(FP8X4),
                scales=z_scales[:].rearrange("p g c -> p (g c)"),
                in_=z_grouped[:].rearrange("p g c t -> p (g c t)"),
            )
            codes_of[group] = z_codes
            scales_of[group] = z_scales

        def multiply(group, tiles):
            for r in tiles:
                if r >= Z_TILES:
                    continue
                acc = psum_acc.tile([P, D_OUT], F32, tag="acc")
                for g in range(PASSES):
                    nc.tensor.matmul_mx(
                        out=acc[:],
                        lhsT=codes_of[group][:, g, r * P : (r + 1) * P].bitcast(FP8X4),
                        lhsT_scale=scales_of[group][:, g, r * P : (r + 1) * P],
                        rhs=w_codes[:, g, :].bitcast(FP8X4),
                        rhs_scale=w_scales[:, g, :],
                        start=(g == 0),
                        stop=(g == PASSES - 1),
                    )
                acc_of[group, r] = acc

        def add_bias(group, r):
            if group not in h_of:
                h = h_pool.tile([P, Z_TILES, D_OUT], F32)
                h_of[group] = h
                sum_squares = small.tile([P, TILES], F32)
                sum_squares_of[group] = sum_squares
            if r < Z_TILES:
                nc.vector.tensor_tensor(
                    out=h_of[group][:, r, :], in0=acc_of[group, r][:], in1=bias_rows[:], op=ALU.add
                )

        def multiply_channels(group, pair):
            if GROUP_TILES[group] < TILES:
                return
            if group not in relu_w_of:
                relu_w = h_pool.tile([P, D_BLOCKS, Z_TILES * P], F32)
                relu_w_of[group] = relu_w
            rows = slice(Z_TILES * P, TILES * P)
            accw = psum_s.tile([P, 2, Z_TILES * P], F32, tag="stream")
            for k in range(2):
                d = 2 * pair + k
                for g in range(PASSES):
                    nc.tensor.matmul_mx(
                        out=accw[:, k, :],
                        lhsT=w_codes[:, g, d * P : (d + 1) * P].bitcast(FP8X4),
                        lhsT_scale=w_scales[:, g, d * P : (d + 1) * P],
                        rhs=codes_of[group][:, g, rows].bitcast(FP8X4),
                        rhs_scale=scales_of[group][:, g, rows],
                        start=(g == 0),
                        stop=(g == PASSES - 1),
                    )
            accw_of[group, pair] = accw

        def relu_channels(group, pair, engine):
            if GROUP_TILES[group] < TILES:
                return
            for k in range(2):
                d = 2 * pair + k
                column = per_partition[:, 2 * BLOCKS + d : 2 * BLOCKS + d + 1]
                if (d in VRELU) != (engine == "V"):
                    continue
                if engine == "V":
                    nc.vector.tensor_scalar(
                        out=relu_w_of[group][:, d, :],
                        in0=accw_of[group, pair][:, k, :],
                        scalar1=column,
                        scalar2=0.0,
                        op0=ALU.add,
                        op1=ALU.max,
                    )
                else:
                    nc.scalar.activation(
                        out=relu_w_of[group][:, d, :],
                        in_=accw_of[group, pair][:, k, :],
                        func=ACT.Relu,
                        bias=column,
                    )

        def rows_back(group):
            if GROUP_TILES[group] < TILES:
                return
            for r in range(Z_TILES, TILES):
                back = psum_back.tile([P, D_BLOCKS, P], F32, tag="back")
                for d in range(D_BLOCKS):
                    nc.tensor.transpose(
                        back[:, d, :],
                        relu_w_of[group][:, d, (r - Z_TILES) * P : (r - Z_TILES + 1) * P],
                        identity[:],
                    )
                back_of[group, r] = back

        def squares_back(group):
            for r in tiles_on(SQ, group, "B"):
                squares = junk_pool.tile([P, D_OUT], BF16, name="squares_back")
                nc.scalar.activation(
                    out=squares[:],
                    in_=back_of[group, r][:].rearrange("p d i -> p (d i)"),
                    func=ACT.Square,
                    accum_out=sum_squares_of[group][:, r : r + 1],
                )

        def units_back(group, engine):
            for r in tiles_on(UN, group, engine):
                if r >= Z_TILES:
                    back = back_of[group, r][:].rearrange("p d i -> p (d i)")
                    scale = inv_norm_of[group][:, r : r + 1]
                    if engine == "V":
                        nc.vector.tensor_scalar_mul(
                            out=unit_of[group][:, r, :], in0=back, scalar1=scale
                        )
                    else:
                        nc.scalar.activation(
                            out=unit_of[group][:, r, :], in_=back, func=ACT.Relu, scale=scale
                        )

        def squares_vector(group, number):
            for r in tiles_on(SQ, group, "V")[number : number + 1]:
                squares = junk_pool.tile([P, D_OUT], BF16)
                nc.vector.scalar_tensor_tensor(
                    out=squares[:],
                    in0=h_of[group][:, r, :],
                    scalar=0.0,
                    in1=h_of[group][:, r, :],
                    op0=ALU.max,
                    op1=ALU.mult,
                    accum_out=sum_squares_of[group][:, r : r + 1],
                )

        def squares_scalar(group):
            tiles = tiles_on(SQ, group, "S")
            for r in tiles:
                relu = h_pool.tile([P, D_OUT], F32, name="relu_%d" % r)
                relu_of[group, r] = relu
                nc.scalar.activation(out=relu[:], in_=h_of[group][:, r, :], func=ACT.Relu)
            for r in tiles:
                squares = junk_pool.tile([P, D_OUT], BF16, name="squares_scalar")
                nc.scalar.activation(
                    out=squares[:],
                    in_=relu_of[group, r][:],
                    func=ACT.Square,
                    accum_out=sum_squares_of[group][:, r : r + 1],
                )

        def inverse_norm(group):
            tiles = GROUP_TILES[group]
            above = small.tile([P, TILES], F32)
            nc.scalar.activation(
                out=above[:, 0:tiles],
                in_=sum_squares_of[group][:, 0:tiles],
                func=ACT.Relu,
                bias=floor[:, 0:1],
            )
            inv_norm = small.tile([P, TILES], F32)
            nc.scalar.activation(
                out=inv_norm[:, 0:tiles],
                in_=above[:, 0:tiles],
                func=ACT.Abs_reciprocal_sqrt,
                bias=floor[:, 1:2],
            )
            inv_norm_of[group] = inv_norm
            unit = o_pool.tile([P, TILES, D_OUT], F32)
            unit_of[group] = unit

        def unit_rows(group, half):
            for r in tiles_on(UN, group, "S"):
                if r < Z_TILES and r // 2 == half:
                    nc.scalar.activation(
                        out=unit_of[group][:, r, :],
                        in_=h_of[group][:, r, :],
                        func=ACT.Relu,
                        scale=inv_norm_of[group][:, r : r + 1],
                    )

        def unit_rows_vector(group):
            for r in [r for r in tiles_on(UN, group, "V") if r < Z_TILES]:
                nc.vector.tensor_scalar(
                    out=unit_of[group][:, r, :],
                    in0=h_of[group][:, r, :],
                    scalar1=0.0,
                    scalar2=inv_norm_of[group][:, r : r + 1],
                    op0=ALU.max,
                    op1=ALU.mult,
                )

        def unit_rows_gpsimd(group):
            for r in tiles_on(UN, group, "G"):
                nc.gpsimd.tensor_scalar(
                    out=unit_of[group][:, r, :],
                    in0=relu_of[group, r][:],
                    scalar1=inv_norm_of[group][:, r : r + 1],
                    scalar2=0.0,
                    op0=ALU.mult,
                    op1=ALU.add,
                )

        def store_unit_rows(group):
            tiles = GROUP_TILES[group]
            nc.sync.dma_start(
                out=out[rows_of(group), :].rearrange("(p r) d -> p r d", r=tiles),
                in_=unit_of[group][:, 0:tiles, :],
            )

        def run(stage, group, *parts):
            if 0 <= group < GROUPS:
                stage(group, *parts)

        for step in range(-FIRST_STAGE_LEAD, GROUPS + LAST_STAGE_LAG + 1):
            if step > -FIRST_STAGE_LEAD:
                run(load_rows, step + FIRST_STAGE_LEAD)
            if step == WEIGHTS_LOAD_STEP:
                load_weights()
            if step == WEIGHTS_LOAD_STEP + 1:
                load_small_vectors()
            run(negate_mean, step + 1)
            run(normalise_gpsimd, step + 1)
            run(row_factors, step + 1)
            for r in range(Z_TILES):
                run(add_bias, step - 3, r)
            run(row_statistics, step + 2)
            run(inverse_norm, step - 4)
            run(transpose_and_scale, step, (0, 1))
            run(units_back, step - 4, "S")
            run(units_back, step - 4, "V")
            run(unit_rows, step - 4, 0)
            run(context_half, step, (0, 1))
            run(multiply, step - 2, (0,))
            run(transpose_and_scale, step, (2, 3))
            run(context_half, step, (2, 3))
            run(multiply, step - 2, (1,))
            run(rows_back, step - 3)
            run(multiply_channels, step - 2, 0)
            run(squares_back, step - 3)
            run(relu_channels, step - 2, 0, "S")
            run(multiply_channels, step - 2, 1)
            run(inverse_std, step + 2)
            run(relu_channels, step - 2, 1, "S")
            run(squares_scalar, step - 3)
            if 0 <= step < PASSES:
                weight_words(step)
            run(group_words, step - 1)
            run(normalise_vector, step + 1)
            run(unit_rows_vector, step - 4)
            run(store_unit_rows, step - 4)
            run(squares_vector, step - 3, 0)
            run(squares_vector, step - 3, 1)
            if 0 <= step < PARTS:
                features_rest(step)
                features_round(step)
            run(quantise, step - 1)
            if step == 1:
                for g in range(PASSES):
                    quantise_weights(g)
            run(context_words, step)
            run(transpose_factors, step + 1)
